import numpy as np
import ml_dtypes


def mxq(x, axis, fmt="e4m3"):
    dtype, down = {"e4m3": (ml_dtypes.float8_e4m3fn, 7), "e5m2": (ml_dtypes.float8_e5m2, 14)}[fmt]
    v = np.moveaxis(np.asarray(x, np.float32).astype(ml_dtypes.bfloat16).astype(np.float64), axis, -1)
    blocks = v.reshape(v.shape[:-1] + (-1, 32))
    amax = np.abs(blocks).max(-1, keepdims=True)
    byte = np.maximum(np.where(amax > 0, np.frexp(amax)[1] - 1 + 127, 0) - down, 1)
    scale = np.exp2(byte - 127.0)
    codes = (blocks / scale).astype(np.float32).astype(dtype).astype(np.float64)
    return np.moveaxis((codes * scale).reshape(v.shape), -1, axis)


WIDE = False


def mx_kscale(k):
    if not WIDE:
        return np.ones(k)
    levels = np.array([10, -10, 5, -5, 0])
    a = np.random.permutation(np.resize(levels, k // 512 * 4)).reshape(k // 512, 4)
    idx = np.arange(k)
    return np.exp2(a[idx // 512, idx % 128 // 32])


BF16 = ml_dtypes.bfloat16


def bf(x):
    return np.asarray(x, np.float32).astype(BF16)


def f64(x):
    return np.asarray(x).astype(np.float64)


B, HALF, MID = 512, 512, 2048
D = 2 * HALF


def setup_inputs():
    s, t = mx_kscale(MID), mx_kscale(MID)
    return {"x": bf(np.random.standard_normal((B, D))),
            "h3": bf(np.maximum(np.random.standard_normal((B, MID)), 0.0) * s),
            "W4": bf(np.random.standard_normal((MID, MID)) * np.sqrt(2.0 / MID) / s[:, None] * t),
            "b4": bf(np.random.standard_normal(MID) * 0.2 * t),
            "W5": bf(np.random.standard_normal((MID, HALF)) * np.sqrt(2.0 / MID) / t[:, None]),
            "b5": bf(np.random.standard_normal(HALF) * 0.2)}


def reference(x, h3, W4, b4, W5, b5):
    x = f64(x)
    even = x[:, 0::2]
    odd = x[:, 1::2]
    h4 = np.maximum((mxq(f64(h3), 1, "e4m3") @ mxq(f64(W4), 0, "e4m3")) + f64(b4), 0.0)
    m = (mxq(h4, 1, "e4m3") @ mxq(f64(W5), 0, "e4m3")) + f64(b5)
    transformed = even + m
    return np.stack([transformed, odd], axis=2).reshape(B, -1)

@@ -1,0 +1,285 @@
+from contextlib import ExitStack
+
+import concourse.mybir as mybir
+from concourse.masks import make_identity
+
+F32 = mybir.dt.float32
+BF16 = mybir.dt.bfloat16
+U32 = mybir.dt.uint32
+U8 = mybir.dt.uint8
+FP8X4 = mybir.dt.float8_e4m3fn_x4
+ACT = mybir.ActivationFunctionType
+ALU = mybir.AluOpType
+
+P = 128
+B = 512
+MID = 2048
+HALF = 512
+KP = 512
+NG = MID // KP
+NBT = B // P
+
+FLOPS = 2 * B * MID * MID + 2 * B * MID * HALF
+
+LOOKAHEAD = 12
+NV_W = 264
+
+
+def regroup(nc, dst, src, width, nv):
+    nc.vector.tensor_copy(
+        out=dst[:, 0:nv, :].rearrange("p (c i) t -> p c t i", i=4),
+        in_=src[:, :, 0:nv].rearrange("p t (c i) -> p c t i", i=4),
+    )
+    if nv < width:
+        nc.scalar.copy(
+            out=dst[:, nv:width, :].rearrange("p (c i) t -> p c t i", i=4),
+            in_=src[:, :, nv:width].rearrange("p t (c i) -> p c t i", i=4),
+        )
+
+
+def tile_additivecoupling_pa_kernel(tc, x, h3, W4, b4, W5, b5, out):
+    nc = tc.nc
+    with ExitStack() as ctx:
+        const = ctx.enter_context(tc.tile_pool(name="const", bufs=1))
+        keep = ctx.enter_context(tc.tile_pool(name="keep", bufs=1))
+        raw4 = ctx.enter_context(tc.tile_pool(name="raw4", bufs=LOOKAHEAD))
+        grp = ctx.enter_context(tc.tile_pool(name="grp", bufs=4))
+        cod4 = ctx.enter_context(tc.tile_pool(name="cod4", bufs=6))
+        h4pool = ctx.enter_context(tc.tile_pool(name="h4pool", bufs=2))
+        opool = ctx.enter_context(tc.tile_pool(name="opool", bufs=8))
+        psa = ctx.enter_context(tc.psum_pool(name="psa", bufs=8))
+
+        ident = const.tile([P, P], F32, name="ident")
+        make_identity(nc, ident[:])
+        identb = const.tile([P, P], BF16, name="identb")
+        nc.vector.tensor_copy(out=identb[:], in_=ident[:])
+
+        brow = const.tile([P, P], BF16, name="brow")
+        nc.vector.memset(brow[:], 0.0)
+        nc.scalar.dma_start(out=brow[0:16, :], in_=b4.rearrange("(r c) -> r c", c=P))
+        nc.scalar.dma_start(out=brow[16:20, :], in_=b5.rearrange("(r c) -> r c", c=P))
+
+        h3r = []
+        for bt in range(NBT):
+            t_ = keep.tile([P, MID], BF16, name="h3r%d" % bt)
+            nc.sync.dma_start(out=t_[:], in_=h3[bt * P : (bt + 1) * P, :])
+            h3r.append(t_)
+
+        w4r = {}
+
+        def load_w4(i):
+            c2, g = divmod(i, NG)
+            r = raw4.tile([P, 4, KP], BF16, name="w4r", tag="w4r")
+            for u in range(2):
+                k0 = g * KP + u * 256
+                nc.sync.dma_start(
+                    out=r[:, 2 * u : 2 * u + 2, :],
+                    in_=W4[k0 : k0 + 256, c2 * KP : (c2 + 1) * KP].rearrange("(q e) c -> q e c", e=2),
+                )
+            w4r[i] = r
+
+        for i in range(LOOKAHEAD):
+            load_w4(i)
+
+        w5r = []
+        xr = []
+
+        def load_tail():
+            for c in range(NG):
+                t_ = keep.tile([P, 4, HALF], BF16, name="w5r%d" % c)
+                nc.sync.dma_start(
+                    out=t_[:], in_=W5[c * KP : (c + 1) * KP, :].rearrange("(t p) j -> p t j", p=P)
+                )
+                w5r.append(t_)
+            for bt in range(NBT):
+                t_ = keep.tile([P, 2 * HALF], BF16, name="xr%d" % bt)
+                nc.sync.dma_start(out=t_[:], in_=x[bt * P : (bt + 1) * P, :])
+                xr.append(t_)
+
+        browf = const.tile([P, P], F32, name="browf")
+        nc.vector.tensor_copy(out=browf[:], in_=brow[:])
+        pb = psa.tile([P, 512], F32, name="pb", tag="a")
+        nc.tensor.transpose(pb[:, 0:P], browf[:], ident[:])
+        bias = const.tile([P, 32], F32, name="bias")
+        nc.vector.tensor_copy(out=bias[:, 0:20], in_=pb[:, 0:20])
+
+        h3g = [keep.tile([P, B, 2], F32, name="h3g%d" % g, align_bytes=64) for g in range(NG)]
+        h3c = keep.tile([P, NG, B], U32, name="h3c", align_bytes=64)
+        h3s = keep.tile([P, NG, B], U8, name="h3s", align_bytes=64)
+        n_exit = 0
+        for half in range(2):
+            for g in range(NG):
+                pt = psa.tile([P, 2, 256], F32, name="pt", tag="a")
+                for h in range(2):
+                    words = h3r[2 * half + h][:].bitcast(F32)
+                    for u in range(2):
+                        w0 = g * 256 + u * P
+                        nc.tensor.transpose(pt[:, u, h * P : (h + 1) * P], words[:, w0 : w0 + P], ident[:])
+                dst = h3g[g][:, half * 256 : (half + 1) * 256, :]
+                src = pt[:].rearrange("p u b -> p b u")
+                if n_exit % 2 == 0:
+                    nc.scalar.copy(out=dst, in_=src)
+                else:
+                    nc.vector.tensor_copy(out=dst, in_=src)
+                n_exit += 1
+        for g in range(NG):
+            nc.vector.quantize_mx(
+                out=h3c[:, g, :].bitcast(FP8X4),
+                scales=h3s[:, g, :],
+                in_=h3g[g][:].rearrange("p b u -> p (b u)").bitcast(BF16),
+            )
+
+        w4g = {}
+        ps1 = {}
+        h4p = {}
+        h4g = {}
+        h4c = [keep.tile([P, B], U32, name="h4c%d" % c, align_bytes=64) for c in range(NG)]
+        h4s = [keep.tile([P, B], U8, name="h4s%d" % c, align_bytes=64) for c in range(NG)]
+
+        def stage_a(i):
+            g_ = grp.tile([P, KP, 4], BF16, name="wg", tag="g", align_bytes=64)
+            regroup(nc, g_, w4r[i], KP, NV_W)
+            w4g[i] = g_
+
+        def stage_b(i):
+            c2, g = divmod(i, NG)
+            codes = cod4.tile([P, KP], U32, name="w4c", tag="w4c", align_bytes=64)
+            scales = cod4.tile([P, KP], U8, name="w4s", tag="w4s", align_bytes=64)
+            nc.vector.quantize_mx(
+                out=codes[:].bitcast(FP8X4),
+                scales=scales[:],
+                in_=w4g[i][:].rearrange("p c t -> p (c t)"),
+            )
+            for t in range(4):
+                if g == 0:
+                    ps1[t] = psa.tile([P, B], F32, name="ps1", tag="a")
+                nc.tensor.matmul_mx(
+                    out=ps1[t][:],
+                    lhsT=codes[:, t * P : (t + 1) * P].bitcast(FP8X4),
+                    lhsT_scale=scales[:, t * P : (t + 1) * P],
+                    rhs=h3c[:, g, :].bitcast(FP8X4),
+                    rhs_scale=h3s[:, g, :],
+                    start=(g == 0),
+                    stop=(g == NG - 1),
+                )
+
+        def stage_c(c2, on_vector):
+            hp = h4pool.tile([P, 4, B], BF16, name="h4p", tag="h4p")
+            for t in range(4):
+                col = bias[:, 4 * c2 + t : 4 * c2 + t + 1]
+                if t in on_vector:
+                    nc.vector.tensor_scalar(
+                        out=hp[:, t, :], in0=ps1[t][:], scalar1=col, scalar2=0.0, op0=ALU.add, op1=ALU.max
+                    )
+                else:
+                    nc.scalar.activation(out=hp[:, t, :], in_=ps1[t][:], func=ACT.Relu, bias=col, scale=1.0)
+            h4p[c2] = hp
+
+        def stage_d(c2, nv):
+            hg = h4pool.tile([P, B, 4], BF16, name="h4g", tag="h4g", align_bytes=64)
+            regroup(nc, hg, h4p[c2], B, nv)
+            h4g[c2] = hg
+
+        def stage_e(c2):
+            nc.vector.quantize_mx(
+                out=h4c[c2][:].bitcast(FP8X4),
+                scales=h4s[c2][:],
+                in_=h4g[c2][:].rearrange("p b t -> p (b t)"),
+            )
+
+        for i in range(4 * NG + 1):
+            if i < 4 * NG:
+                stage_a(i)
+                if i + LOOKAHEAD < 4 * NG:
+                    load_w4(i + LOOKAHEAD)
+                if i + LOOKAHEAD == 4 * NG - 1:
+                    load_tail()
+            if i >= 6 and i % 4 == 2:
+                stage_d(i // 4 - 1, B)
+            if i >= 1:
+                stage_b(i - 1)
+                if (i - 1) % 4 == 3:
+                    last = i == 4 * NG
+                    stage_c((i - 1) // 4, (1, 3) if last else ())
+            if i >= 7 and i % 4 == 3:
+                stage_e(i // 4 - 1)
+
+        w5c = keep.tile([P, NG, HALF], U32, name="w5c", align_bytes=64)
+        w5s = keep.tile([P, NG, HALF], U8, name="w5s", align_bytes=64)
+        w5g = {}
+
+        def stage_a5(c):
+            g_ = grp.tile([P, HALF, 4], BF16, name="wg5", tag="g", align_bytes=64)
+            regroup(nc, g_, w5r[c], HALF, NV_W)
+            w5g[c] = g_
+
+        def stage_q5(c):
+            nc.vector.quantize_mx(
+                out=w5c[:, c, :].bitcast(FP8X4),
+                scales=w5s[:, c, :],
+                in_=w5g[c][:].rearrange("p c t -> p (c t)"),
+            )
+
+        stage_a5(0)
+        stage_a5(1)
+        stage_d(3, 320)
+        stage_q5(0)
+        stage_a5(2)
+        stage_e(3)
+        stage_q5(1)
+        stage_a5(3)
+        stage_q5(2)
+        stage_q5(3)
+
+        acc = [psa.tile([P, B], F32, name="acc%d" % jt, tag="a") for jt in range(4)]
+        for c in range(NG):
+            for jt in range(4):
+                nc.tensor.matmul_mx(
+                    out=acc[jt][:],
+                    lhsT=w5c[:, c, jt * P : (jt + 1) * P].bitcast(FP8X4),
+                    lhsT_scale=w5s[:, c, jt * P : (jt + 1) * P],
+                    rhs=h4c[c][:].bitcast(FP8X4),
+                    rhs_scale=h4s[c][:],
+                    start=(c == 0),
+                    stop=(c == NG - 1),
+                )
+
+        zt = []
+        for jt in range(4):
+            z = keep.tile([P, B], F32, name="zt%d" % jt)
+            col = bias[:, 16 + jt : 17 + jt]
+            if jt % 2 == 0:
+                nc.scalar.activation(out=z[:], in_=acc[jt][:], func=ACT.Identity, bias=col, scale=1.0)
+            else:
+                nc.vector.tensor_scalar(out=z[:], in0=acc[jt][:], scalar1=col, scalar2=None, op0=ALU.add)
+            zt.append(z)
+        n_exit = 0
+        for ch in range(2):
+            for bt in range(NBT):
+                f = psa.tile([P, 2, 256], F32, name="f", tag="a")
+                nc.tensor.matmul(
+                    out=f[:],
+                    lhsT=identb[:],
+                    rhs=xr[bt][:, ch * 512 : (ch + 1) * 512].rearrange("p (j e) -> p e j", e=2),
+                    start=True,
+                    stop=False,
+                )
+                for r in range(2):
+                    nc.tensor.matmul(
+                        out=f[:, 0, r * P : (r + 1) * P],
+                        lhsT=zt[2 * ch + r][:, bt * P : (bt + 1) * P],
+                        rhs=ident[:],
+                        is_transpose=True,
+                        start=False,
+                        stop=(r == 1),
+                    )
+                o = opool.tile([P, 256, 2], F32, name="o", tag="o")
+                if n_exit % 2 == 0:
+                    nc.scalar.copy(out=o[:], in_=f[:].rearrange("p e j -> p j e"))
+                else:
+                    nc.vector.tensor_copy(out=o[:], in_=f[:].rearrange("p e j -> p j e"))
+                n_exit += 1
+                nc.sync.dma_start(
+                    out=out[bt * P : (bt + 1) * P, ch * 512 : (ch + 1) * 512],
+                    in_=o[:].rearrange("p j e -> p (j e)"),
+                )

@@ -22,19 +22,11 @@ NBT = B // P
 FLOPS = 2 * B * MID * MID + 2 * B * MID * HALF
 
 LOOKAHEAD = 12
-NV_W = 264
-
-
-def regroup(nc, dst, src, width, nv):
-    nc.vector.tensor_copy(
-        out=dst[:, 0:nv, :].rearrange("p (c i) t -> p c t i", i=4),
-        in_=src[:, :, 0:nv].rearrange("p t (c i) -> p c t i", i=4),
-    )
-    if nv < width:
-        nc.scalar.copy(
-            out=dst[:, nv:width, :].rearrange("p (c i) t -> p c t i", i=4),
-            in_=src[:, :, nv:width].rearrange("p t (c i) -> p c t i", i=4),
-        )
+NV_W4 = [288,288,256,0,512,288,384,288,288,256,512,352,416,224,0,0]
+NV_H4 = [512,480,512,128]
+NV_W5 = [512,512,0,352]
+ON_VECTOR = ["F3","F5","F7","F0","F6","XH31","XH01","XH00","Z0","X20","XH20"]
+ORDER = [["Db"],["DW4",0],["DW4",1],["Dh3",0],["Dh3",1],["Dh3",2],["Dh3",3],["DW4",2],["DW4",3],["DW4",4],["DW4",5],["DW4",6],["DW4",7],["DW4",8],["DW4",9],["DW4",10],["DW4",11],["TB0"],["Rs",0],["Rv",0],["DW4",12],["Rs",1],["Rv",1],["DW4",13],["Q",0],["TH",0,0],["Q",1],["TH",0,1],["XH",0,0],["TH",1,0],["XH",0,1],["TH",1,1],["XH",1,0],["TH",2,0],["XH",1,1],["Q3",0,0],["TH",2,1],["Q3",1,0],["XH",2,0],["XH",2,1],["TH",3,0],["Q3",2,0],["TH",3,1],["TB1"],["XH",3,0],["Q3",3,0],["XH",3,1],["Rs",2],["Q3",0,1],["Q3",1,1],["L1",0],["Q3",2,1],["Rs",3],["Q3",3,1],["TB2"],["Rv",2],["DW4",14],["DW4",15],["DW5",0],["DW5",1],["DW5",2],["DW5",3],["Dx",0],["Dx",1],["Dx",2],["Dx",3],["L1",1],["Rv",4],["Q",2],["Rs",5],["Q",3],["L1",2],["Q",4],["Rs",6],["Rv",6],["Rs",7],["L1",3],["Rv",5],["X",0,2],["L1",4],["Rv",8],["X",0,3],["Q",5],["Rs",8],["Q",6],["L1",5],["Rv",9],["X",0,1],["Rv",7],["Rs",9],["L1",6],["Q",8],["Q",7],["Rs",11],["Rv",10],["L1",7],["X",0,0],["X",1,0],["Rv",12],["Rs",13],["L1",8],["Q",9],["Q",10],["X",1,3],["L1",9],["Rv",11],["X",1,2],["X",1,1],["RHv",0],["L1",10],["Rs",15],["Q",11],["RHv",1],["L1",11],["Rs",12],["Rv",13],["X",2,2],["Q",12],["X",2,3],["Q",13],["L1",12],["Rs",14],["Q",15],["X",2,0],["L1",13],["QH",0],["R5v",1],["R5s",2],["Q",14],["Q5",1],["L1",14],["R5v",0],["RHs",1],["X",2,1],["L1",15],["QH",1],["R5s",3],["Q5",0],["X",3,2],["RHv",2],["X",3,0],["L2",0],["X",3,3],["Q5",2],["X",3,1],["L2",1],["QH",2],["RHs",3],["R5v",3],["XM",0],["L2",2],["RHv",3],["Q5",3],["XM",1],["QH",3],["XM",2],["XM",3],["L2",3],["Z",0],["Z",1],["XM",4],["Z",3],["XM",5],["TF",0],["Z",2],["TF",1],["F",0],["XM",7],["TF",2],["F",1],["TF",3],["XM",6],["F",3],["TF",4],["F",2],["TF",5],["TF",6],["F",5],["TF",7],["F",4],["F",6],["F",7]]
 
 
 def tile_additivecoupling_pa_kernel(tc, x, h3, W4, b4, W5, b5, out):
@@ -43,243 +35,207 @@ def tile_additivecoupling_pa_kernel(tc, x, h3, W4, b4, W5, b5, out):
         const = ctx.enter_context(tc.tile_pool(name="const", bufs=1))
         keep = ctx.enter_context(tc.tile_pool(name="keep", bufs=1))
         raw4 = ctx.enter_context(tc.tile_pool(name="raw4", bufs=LOOKAHEAD))
-        grp = ctx.enter_context(tc.tile_pool(name="grp", bufs=4))
+        grp = ctx.enter_context(tc.tile_pool(name="grp", bufs=5))
         cod4 = ctx.enter_context(tc.tile_pool(name="cod4", bufs=6))
         h4pool = ctx.enter_context(tc.tile_pool(name="h4pool", bufs=2))
         opool = ctx.enter_context(tc.tile_pool(name="opool", bufs=8))
         psa = ctx.enter_context(tc.psum_pool(name="psa", bufs=8))
+        ctx.enter_context(tc.manual_schedule())
 
+        brow = const.tile([P, P], BF16, name="brow")
+        nc.vector.memset(brow[:], 0.0)
         ident = const.tile([P, P], F32, name="ident")
         make_identity(nc, ident[:])
         identb = const.tile([P, P], BF16, name="identb")
         nc.vector.tensor_copy(out=identb[:], in_=ident[:])
-
-        brow = const.tile([P, P], BF16, name="brow")
-        nc.vector.memset(brow[:], 0.0)
-        nc.scalar.dma_start(out=brow[0:16, :], in_=b4.rearrange("(r c) -> r c", c=P))
-        nc.scalar.dma_start(out=brow[16:20, :], in_=b5.rearrange("(r c) -> r c", c=P))
-
-        h3r = []
-        for bt in range(NBT):
-            t_ = keep.tile([P, MID], BF16, name="h3r%d" % bt)
-            nc.sync.dma_start(out=t_[:], in_=h3[bt * P : (bt + 1) * P, :])
-            h3r.append(t_)
-
-        w4r = {}
-
-        def load_w4(i):
-            c2, g = divmod(i, NG)
-            r = raw4.tile([P, 4, KP], BF16, name="w4r", tag="w4r")
-            for u in range(2):
-                k0 = g * KP + u * 256
-                nc.sync.dma_start(
-                    out=r[:, 2 * u : 2 * u + 2, :],
-                    in_=W4[k0 : k0 + 256, c2 * KP : (c2 + 1) * KP].rearrange("(q e) c -> q e c", e=2),
-                )
-            w4r[i] = r
-
-        for i in range(LOOKAHEAD):
-            load_w4(i)
-
-        w5r = []
-        xr = []
-
-        def load_tail():
-            for c in range(NG):
-                t_ = keep.tile([P, 4, HALF], BF16, name="w5r%d" % c)
-                nc.sync.dma_start(
-                    out=t_[:], in_=W5[c * KP : (c + 1) * KP, :].rearrange("(t p) j -> p t j", p=P)
-                )
-                w5r.append(t_)
-            for bt in range(NBT):
-                t_ = keep.tile([P, 2 * HALF], BF16, name="xr%d" % bt)
-                nc.sync.dma_start(out=t_[:], in_=x[bt * P : (bt + 1) * P, :])
-                xr.append(t_)
-
         browf = const.tile([P, P], F32, name="browf")
-        nc.vector.tensor_copy(out=browf[:], in_=brow[:])
-        pb = psa.tile([P, 512], F32, name="pb", tag="a")
-        nc.tensor.transpose(pb[:, 0:P], browf[:], ident[:])
         bias = const.tile([P, 32], F32, name="bias")
-        nc.vector.tensor_copy(out=bias[:, 0:20], in_=pb[:, 0:20])
 
-        h3g = [keep.tile([P, B, 2], F32, name="h3g%d" % g, align_bytes=64) for g in range(NG)]
+        h3r = [keep.tile([P, MID], BF16, name="h3r%d" % bt) for bt in range(NBT)]
+        w5r = [keep.tile([P, 4, HALF], BF16, name="w5r%d" % c) for c in range(NG)]
+        xr = [keep.tile([P, 2 * HALF], BF16, name="xr%d" % bt) for bt in range(NBT)]
+        h3g = keep.tile([P, NG, B, 2], F32, name="h3g", align_bytes=64)
         h3c = keep.tile([P, NG, B], U32, name="h3c", align_bytes=64)
         h3s = keep.tile([P, NG, B], U8, name="h3s", align_bytes=64)
-        n_exit = 0
-        for half in range(2):
-            for g in range(NG):
-                pt = psa.tile([P, 2, 256], F32, name="pt", tag="a")
-                for h in range(2):
-                    words = h3r[2 * half + h][:].bitcast(F32)
-                    for u in range(2):
-                        w0 = g * 256 + u * P
-                        nc.tensor.transpose(pt[:, u, h * P : (h + 1) * P], words[:, w0 : w0 + P], ident[:])
-                dst = h3g[g][:, half * 256 : (half + 1) * 256, :]
-                src = pt[:].rearrange("p u b -> p b u")
-                if n_exit % 2 == 0:
-                    nc.scalar.copy(out=dst, in_=src)
-                else:
-                    nc.vector.tensor_copy(out=dst, in_=src)
-                n_exit += 1
-        for g in range(NG):
-            nc.vector.quantize_mx(
-                out=h3c[:, g, :].bitcast(FP8X4),
-                scales=h3s[:, g, :],
-                in_=h3g[g][:].rearrange("p b u -> p (b u)").bitcast(BF16),
-            )
-
-        w4g = {}
-        ps1 = {}
-        h4p = {}
-        h4g = {}
         h4c = [keep.tile([P, B], U32, name="h4c%d" % c, align_bytes=64) for c in range(NG)]
         h4s = [keep.tile([P, B], U8, name="h4s%d" % c, align_bytes=64) for c in range(NG)]
-
-        def stage_a(i):
-            g_ = grp.tile([P, KP, 4], BF16, name="wg", tag="g", align_bytes=64)
-            regroup(nc, g_, w4r[i], KP, NV_W)
-            w4g[i] = g_
-
-        def stage_b(i):
-            c2, g = divmod(i, NG)
-            codes = cod4.tile([P, KP], U32, name="w4c", tag="w4c", align_bytes=64)
-            scales = cod4.tile([P, KP], U8, name="w4s", tag="w4s", align_bytes=64)
-            nc.vector.quantize_mx(
-                out=codes[:].bitcast(FP8X4),
-                scales=scales[:],
-                in_=w4g[i][:].rearrange("p c t -> p (c t)"),
-            )
-            for t in range(4):
-                if g == 0:
-                    ps1[t] = psa.tile([P, B], F32, name="ps1", tag="a")
-                nc.tensor.matmul_mx(
-                    out=ps1[t][:],
-                    lhsT=codes[:, t * P : (t + 1) * P].bitcast(FP8X4),
-                    lhsT_scale=scales[:, t * P : (t + 1) * P],
-                    rhs=h3c[:, g, :].bitcast(FP8X4),
-                    rhs_scale=h3s[:, g, :],
-                    start=(g == 0),
-                    stop=(g == NG - 1),
-                )
-
-        def stage_c(c2, on_vector):
-            hp = h4pool.tile([P, 4, B], BF16, name="h4p", tag="h4p")
-            for t in range(4):
-                col = bias[:, 4 * c2 + t : 4 * c2 + t + 1]
-                if t in on_vector:
-                    nc.vector.tensor_scalar(
-                        out=hp[:, t, :], in0=ps1[t][:], scalar1=col, scalar2=0.0, op0=ALU.add, op1=ALU.max
-                    )
-                else:
-                    nc.scalar.activation(out=hp[:, t, :], in_=ps1[t][:], func=ACT.Relu, bias=col, scale=1.0)
-            h4p[c2] = hp
-
-        def stage_d(c2, nv):
-            hg = h4pool.tile([P, B, 4], BF16, name="h4g", tag="h4g", align_bytes=64)
-            regroup(nc, hg, h4p[c2], B, nv)
-            h4g[c2] = hg
-
-        def stage_e(c2):
-            nc.vector.quantize_mx(
-                out=h4c[c2][:].bitcast(FP8X4),
-                scales=h4s[c2][:],
-                in_=h4g[c2][:].rearrange("p b t -> p (b t)"),
-            )
-
-        for i in range(4 * NG + 1):
-            if i < 4 * NG:
-                stage_a(i)
-                if i + LOOKAHEAD < 4 * NG:
-                    load_w4(i + LOOKAHEAD)
-                if i + LOOKAHEAD == 4 * NG - 1:
-                    load_tail()
-            if i >= 6 and i % 4 == 2:
-                stage_d(i // 4 - 1, B)
-            if i >= 1:
-                stage_b(i - 1)
-                if (i - 1) % 4 == 3:
-                    last = i == 4 * NG
-                    stage_c((i - 1) // 4, (1, 3) if last else ())
-            if i >= 7 and i % 4 == 3:
-                stage_e(i // 4 - 1)
-
         w5c = keep.tile([P, NG, HALF], U32, name="w5c", align_bytes=64)
         w5s = keep.tile([P, NG, HALF], U8, name="w5s", align_bytes=64)
-        w5g = {}
+        zt = [keep.tile([P, B], F32, name="zt%d" % jt) for jt in range(4)]
+        live = {}
 
-        def stage_a5(c):
-            g_ = grp.tile([P, HALF, 4], BF16, name="wg5", tag="g", align_bytes=64)
-            regroup(nc, g_, w5r[c], HALF, NV_W)
-            w5g[c] = g_
-
-        def stage_q5(c):
-            nc.vector.quantize_mx(
-                out=w5c[:, c, :].bitcast(FP8X4),
-                scales=w5s[:, c, :],
-                in_=w5g[c][:].rearrange("p c t -> p (c t)"),
-            )
-
-        stage_a5(0)
-        stage_a5(1)
-        stage_d(3, 320)
-        stage_q5(0)
-        stage_a5(2)
-        stage_e(3)
-        stage_q5(1)
-        stage_a5(3)
-        stage_q5(2)
-        stage_q5(3)
-
-        acc = [psa.tile([P, B], F32, name="acc%d" % jt, tag="a") for jt in range(4)]
-        for c in range(NG):
-            for jt in range(4):
-                nc.tensor.matmul_mx(
-                    out=acc[jt][:],
-                    lhsT=w5c[:, c, jt * P : (jt + 1) * P].bitcast(FP8X4),
-                    lhsT_scale=w5s[:, c, jt * P : (jt + 1) * P],
-                    rhs=h4c[c][:].bitcast(FP8X4),
-                    rhs_scale=h4s[c][:],
-                    start=(c == 0),
-                    stop=(c == NG - 1),
-                )
-
-        zt = []
-        for jt in range(4):
-            z = keep.tile([P, B], F32, name="zt%d" % jt)
-            col = bias[:, 16 + jt : 17 + jt]
-            if jt % 2 == 0:
-                nc.scalar.activation(out=z[:], in_=acc[jt][:], func=ACT.Identity, bias=col, scale=1.0)
+        def part(eng, dst, src, lo, hi):
+            o_ = dst[:, lo:hi, :].rearrange("p (c i) t -> p c t i", i=4)
+            i_ = src[:, :, lo:hi].rearrange("p t (c i) -> p c t i", i=4)
+            if eng == "v":
+                nc.vector.tensor_copy(out=o_, in_=i_)
             else:
-                nc.vector.tensor_scalar(out=z[:], in0=acc[jt][:], scalar1=col, scalar2=None, op0=ALU.add)
-            zt.append(z)
-        n_exit = 0
-        for ch in range(2):
-            for bt in range(NBT):
+                nc.scalar.copy(out=o_, in_=i_)
+
+        def grouped(key, tag, pool):
+            if key not in live:
+                live[key] = pool.tile([P, 512, 4], BF16, name=tag, tag=tag, align_bytes=64)
+            return live[key]
+
+        def leave(name, out_ap, in_ap):
+            if name in ON_VECTOR:
+                nc.vector.tensor_copy(out=out_ap, in_=in_ap)
+            else:
+                nc.scalar.copy(out=out_ap, in_=in_ap)
+
+        def run(op):
+            kind = op[0]
+            a = op[1] if len(op) > 1 else 0
+            b_ = op[2] if len(op) > 2 else 0
+            if kind == "Db":
+                nc.sync.dma_start(out=brow[0:16, :], in_=b4.rearrange("(r c) -> r c", c=P))
+                nc.sync.dma_start(out=brow[16:20, :], in_=b5.rearrange("(r c) -> r c", c=P))
+            elif kind == "Dh3":
+                nc.sync.dma_start(out=h3r[a][:], in_=h3[a * P : (a + 1) * P, :])
+            elif kind == "DW4":
+                c2, g = divmod(a, NG)
+                r = raw4.tile([P, 4, KP], BF16, name="w4r", tag="w4r")
+                for u in range(2):
+                    k0 = g * KP + u * 256
+                    nc.sync.dma_start(
+                        out=r[:, 2 * u : 2 * u + 2, :],
+                        in_=W4[k0 : k0 + 256, c2 * KP : (c2 + 1) * KP].rearrange("(q e) c -> q e c", e=2),
+                    )
+                live[("w4r", a)] = r
+            elif kind == "DW5":
+                nc.sync.dma_start(out=w5r[a][:], in_=W5[a * KP : (a + 1) * KP, :].rearrange("(t p) j -> p t j", p=P))
+            elif kind == "Dx":
+                nc.sync.dma_start(out=xr[a][:], in_=x[a * P : (a + 1) * P, :])
+            elif kind == "TB0":
+                nc.vector.tensor_copy(out=browf[:], in_=brow[:])
+            elif kind == "TB1":
+                live["pb"] = psa.tile([P, 512], F32, name="pb", tag="a")
+                nc.tensor.transpose(live["pb"][:, 0:P], browf[:], ident[:])
+            elif kind == "TB2":
+                nc.vector.tensor_copy(out=bias[:, 0:20], in_=live["pb"][:, 0:20])
+            elif kind == "TH":
+                pt = psa.tile([P, 2, 2, P], F32, name="pt", tag="a")
+                words = h3r[a][:].bitcast(F32)
+                for gg in range(2):
+                    for u in range(2):
+                        w0 = (2 * b_ + gg) * 256 + u * P
+                        nc.tensor.transpose(pt[:, gg, u, :], words[:, w0 : w0 + P], ident[:])
+                live[("pt", a, b_)] = pt
+            elif kind == "XH":
+                leave(
+                    "XH%d%d" % (a, b_),
+                    h3g[:, 2 * b_ : 2 * b_ + 2, a * P : (a + 1) * P, :],
+                    live[("pt", a, b_)][:].rearrange("p g u b -> p g b u"),
+                )
+            elif kind == "Q3":
+                nc.vector.quantize_mx(
+                    out=h3c[:, a, b_ * 256 : (b_ + 1) * 256].bitcast(FP8X4),
+                    scales=h3s[:, a, b_ * 256 : (b_ + 1) * 256],
+                    in_=h3g[:, a, b_ * 256 : (b_ + 1) * 256, :].rearrange("p b u -> p (b u)").bitcast(BF16),
+                )
+            elif kind == "Rv":
+                part("v", grouped(("g4", a), "wg", grp), live[("w4r", a)], 0, NV_W4[a])
+            elif kind == "Rs":
+                part("s", grouped(("g4", a), "wg", grp), live[("w4r", a)], NV_W4[a], 512)
+            elif kind == "Q":
+                codes = cod4.tile([P, KP], U32, name="w4c", tag="w4c", align_bytes=64)
+                scales = cod4.tile([P, KP], U8, name="w4s", tag="w4s", align_bytes=64)
+                nc.vector.quantize_mx(
+                    out=codes[:].bitcast(FP8X4), scales=scales[:], in_=live[("g4", a)][:].rearrange("p c t -> p (c t)")
+                )
+                live[("c4", a)] = (codes, scales)
+            elif kind == "L1":
+                c2, g = divmod(a, NG)
+                codes, scales = live[("c4", a)]
+                for t in range(4):
+                    if g == 0:
+                        live[("ps1", c2, t)] = psa.tile([P, B], F32, name="ps1", tag="a")
+                    nc.tensor.matmul_mx(
+                        out=live[("ps1", c2, t)][:],
+                        lhsT=codes[:, t * P : (t + 1) * P].bitcast(FP8X4),
+                        lhsT_scale=scales[:, t * P : (t + 1) * P],
+                        rhs=h3c[:, g, :].bitcast(FP8X4),
+                        rhs_scale=h3s[:, g, :],
+                        start=(g == 0),
+                        stop=(g == NG - 1),
+                    )
+            elif kind == "X":
+                if ("h4p", a) not in live:
+                    live[("h4p", a)] = h4pool.tile([P, 4, B], BF16, name="h4p", tag="h4p")
+                col = bias[:, 4 * a + b_ : 4 * a + b_ + 1]
+                if ("X%d%d" % (a, b_)) in ON_VECTOR:
+                    nc.vector.tensor_scalar(
+                        out=live[("h4p", a)][:, b_, :], in0=live[("ps1", a, b_)][:],
+                        scalar1=col, scalar2=0.0, op0=ALU.add, op1=ALU.max,
+                    )
+                else:
+                    nc.scalar.activation(
+                        out=live[("h4p", a)][:, b_, :], in_=live[("ps1", a, b_)][:], func=ACT.Relu, bias=col, scale=1.0
+                    )
+            elif kind == "RHv":
+                part("v", grouped(("gh", a), "h4g", h4pool), live[("h4p", a)], 0, NV_H4[a])
+            elif kind == "RHs":
+                part("s", grouped(("gh", a), "h4g", h4pool), live[("h4p", a)], NV_H4[a], 512)
+            elif kind == "QH":
+                nc.vector.quantize_mx(
+                    out=h4c[a][:].bitcast(FP8X4), scales=h4s[a][:], in_=live[("gh", a)][:].rearrange("p b t -> p (b t)")
+                )
+            elif kind == "R5v":
+                part("v", grouped(("g5", a), "wg", grp), w5r[a], 0, NV_W5[a])
+            elif kind == "R5s":
+                part("s", grouped(("g5", a), "wg", grp), w5r[a], NV_W5[a], 512)
+            elif kind == "Q5":
+                nc.vector.quantize_mx(
+                    out=w5c[:, a, :].bitcast(FP8X4), scales=w5s[:, a, :], in_=live[("g5", a)][:].rearrange("p c t -> p (c t)")
+                )
+            elif kind == "L2":
+                first = "acc" not in live
+                if first:
+                    live["acc"] = [psa.tile([P, B], F32, name="acc%d" % jt, tag="a") for jt in range(4)]
+                    live["nl2"] = 0
+                live["nl2"] += 1
+                for jt in range(4):
+                    nc.tensor.matmul_mx(
+                        out=live["acc"][jt][:],
+                        lhsT=w5c[:, a, jt * P : (jt + 1) * P].bitcast(FP8X4),
+                        lhsT_scale=w5s[:, a, jt * P : (jt + 1) * P],
+                        rhs=h4c[a][:].bitcast(FP8X4),
+                        rhs_scale=h4s[a][:],
+                        start=first,
+                        stop=(live["nl2"] == NG),
+                    )
+            elif kind == "Z":
+                col = bias[:, 16 + a : 17 + a]
+                if ("Z%d" % a) in ON_VECTOR:
+                    nc.vector.tensor_scalar(out=zt[a][:], in0=live["acc"][a][:], scalar1=col, scalar2=None, op0=ALU.add)
+                else:
+                    nc.scalar.activation(out=zt[a][:], in_=live["acc"][a][:], func=ACT.Identity, bias=col, scale=1.0)
+            elif kind == "XM":
+                ch, bt = divmod(a, NBT)
                 f = psa.tile([P, 2, 256], F32, name="f", tag="a")
                 nc.tensor.matmul(
-                    out=f[:],
-                    lhsT=identb[:],
+                    out=f[:], lhsT=identb[:],
                     rhs=xr[bt][:, ch * 512 : (ch + 1) * 512].rearrange("p (j e) -> p e j", e=2),
-                    start=True,
-                    stop=False,
+                    start=True, stop=False,
                 )
+                live[("f", a)] = f
+            elif kind == "TF":
+                ch, bt = divmod(a, NBT)
                 for r in range(2):
                     nc.tensor.matmul(
-                        out=f[:, 0, r * P : (r + 1) * P],
+                        out=live[("f", a)][:, 0, r * P : (r + 1) * P],
                         lhsT=zt[2 * ch + r][:, bt * P : (bt + 1) * P],
-                        rhs=ident[:],
-                        is_transpose=True,
-                        start=False,
-                        stop=(r == 1),
+                        rhs=ident[:], is_transpose=True, start=False, stop=(r == 1),
                     )
+            elif kind == "F":
+                ch, bt = divmod(a, NBT)
                 o = opool.tile([P, 256, 2], F32, name="o", tag="o")
-                if n_exit % 2 == 0:
-                    nc.scalar.copy(out=o[:], in_=f[:].rearrange("p e j -> p j e"))
-                else:
-                    nc.vector.tensor_copy(out=o[:], in_=f[:].rearrange("p e j -> p j e"))
-                n_exit += 1
+                leave("F%d" % a, o[:], live[("f", a)][:].rearrange("p e j -> p j e"))
                 nc.sync.dma_start(
-                    out=out[bt * P : (bt + 1) * P, ch * 512 : (ch + 1) * 512],
-                    in_=o[:].rearrange("p j e -> p (j e)"),
+                    out=out[bt * P : (bt + 1) * P, ch * 512 : (ch + 1) * 512], in_=o[:].rearrange("p j e -> p (j e)")
                 )
+            else:
+                assert False, kind
+
+        for op in ORDER:
+            run(op)

@@ -22,11 +22,19 @@ NBT = B // P
 FLOPS = 2 * B * MID * MID + 2 * B * MID * HALF
 
 LOOKAHEAD = 12
-NV_W4 = [288,288,256,0,512,288,384,288,288,256,512,352,416,224,0,0]
-NV_H4 = [512,480,512,128]
-NV_W5 = [512,512,0,352]
-ON_VECTOR = ["F3","F5","F7","F0","F6","XH31","XH01","XH00","Z0","X20","XH20"]
-ORDER = [["Db"],["DW4",0],["DW4",1],["Dh3",0],["Dh3",1],["Dh3",2],["Dh3",3],["DW4",2],["DW4",3],["DW4",4],["DW4",5],["DW4",6],["DW4",7],["DW4",8],["DW4",9],["DW4",10],["DW4",11],["TB0"],["Rs",0],["Rv",0],["DW4",12],["Rs",1],["Rv",1],["DW4",13],["Q",0],["TH",0,0],["Q",1],["TH",0,1],["XH",0,0],["TH",1,0],["XH",0,1],["TH",1,1],["XH",1,0],["TH",2,0],["XH",1,1],["Q3",0,0],["TH",2,1],["Q3",1,0],["XH",2,0],["XH",2,1],["TH",3,0],["Q3",2,0],["TH",3,1],["TB1"],["XH",3,0],["Q3",3,0],["XH",3,1],["Rs",2],["Q3",0,1],["Q3",1,1],["L1",0],["Q3",2,1],["Rs",3],["Q3",3,1],["TB2"],["Rv",2],["DW4",14],["DW4",15],["DW5",0],["DW5",1],["DW5",2],["DW5",3],["Dx",0],["Dx",1],["Dx",2],["Dx",3],["L1",1],["Rv",4],["Q",2],["Rs",5],["Q",3],["L1",2],["Q",4],["Rs",6],["Rv",6],["Rs",7],["L1",3],["Rv",5],["X",0,2],["L1",4],["Rv",8],["X",0,3],["Q",5],["Rs",8],["Q",6],["L1",5],["Rv",9],["X",0,1],["Rv",7],["Rs",9],["L1",6],["Q",8],["Q",7],["Rs",11],["Rv",10],["L1",7],["X",0,0],["X",1,0],["Rv",12],["Rs",13],["L1",8],["Q",9],["Q",10],["X",1,3],["L1",9],["Rv",11],["X",1,2],["X",1,1],["RHv",0],["L1",10],["Rs",15],["Q",11],["RHv",1],["L1",11],["Rs",12],["Rv",13],["X",2,2],["Q",12],["X",2,3],["Q",13],["L1",12],["Rs",14],["Q",15],["X",2,0],["L1",13],["QH",0],["R5v",1],["R5s",2],["Q",14],["Q5",1],["L1",14],["R5v",0],["RHs",1],["X",2,1],["L1",15],["QH",1],["R5s",3],["Q5",0],["X",3,2],["RHv",2],["X",3,0],["L2",0],["X",3,3],["Q5",2],["X",3,1],["L2",1],["QH",2],["RHs",3],["R5v",3],["XM",0],["L2",2],["RHv",3],["Q5",3],["XM",1],["QH",3],["XM",2],["XM",3],["L2",3],["Z",0],["Z",1],["XM",4],["Z",3],["XM",5],["TF",0],["Z",2],["TF",1],["F",0],["XM",7],["TF",2],["F",1],["TF",3],["XM",6],["F",3],["TF",4],["F",2],["TF",5],["TF",6],["F",5],["TF",7],["F",4],["F",6],["F",7]]
+NV_W = 264
+
+
+def regroup(nc, dst, src, width, nv):
+    nc.vector.tensor_copy(
+        out=dst[:, 0:nv, :].rearrange("p (c i) t -> p c t i", i=4),
+        in_=src[:, :, 0:nv].rearrange("p t (c i) -> p c t i", i=4),
+    )
+    if nv < width:
+        nc.scalar.copy(
+            out=dst[:, nv:width, :].rearrange("p (c i) t -> p c t i", i=4),
+            in_=src[:, :, nv:width].rearrange("p t (c i) -> p c t i", i=4),
+        )
 
 
 def tile_additivecoupling_pa_kernel(tc, x, h3, W4, b4, W5, b5, out):
@@ -35,207 +43,243 @@ def tile_additivecoupling_pa_kernel(tc, x, h3, W4, b4, W5, b5, out):
         const = ctx.enter_context(tc.tile_pool(name="const", bufs=1))
         keep = ctx.enter_context(tc.tile_pool(name="keep", bufs=1))
         raw4 = ctx.enter_context(tc.tile_pool(name="raw4", bufs=LOOKAHEAD))
-        grp = ctx.enter_context(tc.tile_pool(name="grp", bufs=5))
+        grp = ctx.enter_context(tc.tile_pool(name="grp", bufs=4))
         cod4 = ctx.enter_context(tc.tile_pool(name="cod4", bufs=6))
         h4pool = ctx.enter_context(tc.tile_pool(name="h4pool", bufs=2))
         opool = ctx.enter_context(tc.tile_pool(name="opool", bufs=8))
         psa = ctx.enter_context(tc.psum_pool(name="psa", bufs=8))
-        ctx.enter_context(tc.manual_schedule())
 
-        brow = const.tile([P, P], BF16, name="brow")
-        nc.vector.memset(brow[:], 0.0)
         ident = const.tile([P, P], F32, name="ident")
         make_identity(nc, ident[:])
         identb = const.tile([P, P], BF16, name="identb")
         nc.vector.tensor_copy(out=identb[:], in_=ident[:])
-        browf = const.tile([P, P], F32, name="browf")
-        bias = const.tile([P, 32], F32, name="bias")
 
-        h3r = [keep.tile([P, MID], BF16, name="h3r%d" % bt) for bt in range(NBT)]
-        w5r = [keep.tile([P, 4, HALF], BF16, name="w5r%d" % c) for c in range(NG)]
-        xr = [keep.tile([P, 2 * HALF], BF16, name="xr%d" % bt) for bt in range(NBT)]
+        brow = const.tile([P, P], BF16, name="brow")
+        nc.vector.memset(brow[:], 0.0)
+        nc.sync.dma_start(out=brow[0:16, :], in_=b4.rearrange("(r c) -> r c", c=P))
+        nc.sync.dma_start(out=brow[16:20, :], in_=b5.rearrange("(r c) -> r c", c=P))
+
+        h3r = []
+        for bt in range(NBT):
+            t_ = keep.tile([P, MID], BF16, name="h3r%d" % bt)
+            nc.sync.dma_start(out=t_[:], in_=h3[bt * P : (bt + 1) * P, :])
+            h3r.append(t_)
+
+        w4r = {}
+
+        def load_w4(i):
+            c2, g = divmod(i, NG)
+            r = raw4.tile([P, 4, KP], BF16, name="w4r", tag="w4r")
+            for u in range(2):
+                k0 = g * KP + u * 256
+                nc.sync.dma_start(
+                    out=r[:, 2 * u : 2 * u + 2, :],
+                    in_=W4[k0 : k0 + 256, c2 * KP : (c2 + 1) * KP].rearrange("(q e) c -> q e c", e=2),
+                )
+            w4r[i] = r
+
+        for i in range(LOOKAHEAD):
+            load_w4(i)
+
+        w5r = []
+        xr = []
+
+        def load_tail():
+            for c in range(NG):
+                t_ = keep.tile([P, 4, HALF], BF16, name="w5r%d" % c)
+                nc.sync.dma_start(
+                    out=t_[:], in_=W5[c * KP : (c + 1) * KP, :].rearrange("(t p) j -> p t j", p=P)
+                )
+                w5r.append(t_)
+            for bt in range(NBT):
+                t_ = keep.tile([P, 2 * HALF], BF16, name="xr%d" % bt)
+                nc.sync.dma_start(out=t_[:], in_=x[bt * P : (bt + 1) * P, :])
+                xr.append(t_)
+
         h3g = keep.tile([P, NG, B, 2], F32, name="h3g", align_bytes=64)
         h3c = keep.tile([P, NG, B], U32, name="h3c", align_bytes=64)
         h3s = keep.tile([P, NG, B], U8, name="h3s", align_bytes=64)
-        h4c = [keep.tile([P, B], U32, name="h4c%d" % c, align_bytes=64) for c in range(NG)]
-        h4s = [keep.tile([P, B], U8, name="h4s%d" % c, align_bytes=64) for c in range(NG)]
-        w5c = keep.tile([P, NG, HALF], U32, name="w5c", align_bytes=64)
-        w5s = keep.tile([P, NG, HALF], U8, name="w5s", align_bytes=64)
-        zt = [keep.tile([P, B], F32, name="zt%d" % jt) for jt in range(4)]
-        live = {}
-
-        def part(eng, dst, src, lo, hi):
-            o_ = dst[:, lo:hi, :].rearrange("p (c i) t -> p c t i", i=4)
-            i_ = src[:, :, lo:hi].rearrange("p t (c i) -> p c t i", i=4)
-            if eng == "v":
-                nc.vector.tensor_copy(out=o_, in_=i_)
-            else:
-                nc.scalar.copy(out=o_, in_=i_)
-
-        def grouped(key, tag, pool):
-            if key not in live:
-                live[key] = pool.tile([P, 512, 4], BF16, name=tag, tag=tag, align_bytes=64)
-            return live[key]
-
-        def leave(name, out_ap, in_ap):
-            if name in ON_VECTOR:
-                nc.vector.tensor_copy(out=out_ap, in_=in_ap)
-            else:
-                nc.scalar.copy(out=out_ap, in_=in_ap)
-
-        def run(op):
-            kind = op[0]
-            a = op[1] if len(op) > 1 else 0
-            b_ = op[2] if len(op) > 2 else 0
-            if kind == "Db":
-                nc.sync.dma_start(out=brow[0:16, :], in_=b4.rearrange("(r c) -> r c", c=P))
-                nc.sync.dma_start(out=brow[16:20, :], in_=b5.rearrange("(r c) -> r c", c=P))
-            elif kind == "Dh3":
-                nc.sync.dma_start(out=h3r[a][:], in_=h3[a * P : (a + 1) * P, :])
-            elif kind == "DW4":
-                c2, g = divmod(a, NG)
-                r = raw4.tile([P, 4, KP], BF16, name="w4r", tag="w4r")
-                for u in range(2):
-                    k0 = g * KP + u * 256
-                    nc.sync.dma_start(
-                        out=r[:, 2 * u : 2 * u + 2, :],
-                        in_=W4[k0 : k0 + 256, c2 * KP : (c2 + 1) * KP].rearrange("(q e) c -> q e c", e=2),
-                    )
-                live[("w4r", a)] = r
-            elif kind == "DW5":
-                nc.sync.dma_start(out=w5r[a][:], in_=W5[a * KP : (a + 1) * KP, :].rearrange("(t p) j -> p t j", p=P))
-            elif kind == "Dx":
-                nc.sync.dma_start(out=xr[a][:], in_=x[a * P : (a + 1) * P, :])
-            elif kind == "TB0":
-                nc.vector.tensor_copy(out=browf[:], in_=brow[:])
-            elif kind == "TB1":
-                live["pb"] = psa.tile([P, 512], F32, name="pb", tag="a")
-                nc.tensor.transpose(live["pb"][:, 0:P], browf[:], ident[:])
-            elif kind == "TB2":
-                nc.vector.tensor_copy(out=bias[:, 0:20], in_=live["pb"][:, 0:20])
-            elif kind == "TH":
+        n_exit = 0
+        for bt in range(NBT):
+            words = h3r[bt][:].bitcast(F32)
+            for gp in range(2):
                 pt = psa.tile([P, 2, 2, P], F32, name="pt", tag="a")
-                words = h3r[a][:].bitcast(F32)
                 for gg in range(2):
                     for u in range(2):
-                        w0 = (2 * b_ + gg) * 256 + u * P
+                        w0 = (2 * gp + gg) * 256 + u * P
                         nc.tensor.transpose(pt[:, gg, u, :], words[:, w0 : w0 + P], ident[:])
-                live[("pt", a, b_)] = pt
-            elif kind == "XH":
-                leave(
-                    "XH%d%d" % (a, b_),
-                    h3g[:, 2 * b_ : 2 * b_ + 2, a * P : (a + 1) * P, :],
-                    live[("pt", a, b_)][:].rearrange("p g u b -> p g b u"),
+                dst = h3g[:, 2 * gp : 2 * gp + 2, bt * P : (bt + 1) * P, :]
+                src = pt[:].rearrange("p g u b -> p g b u")
+                if n_exit % 2 == 0:
+                    nc.scalar.copy(out=dst, in_=src)
+                else:
+                    nc.vector.tensor_copy(out=dst, in_=src)
+                n_exit += 1
+        for g in range(NG):
+            nc.vector.quantize_mx(
+                out=h3c[:, g, :].bitcast(FP8X4),
+                scales=h3s[:, g, :],
+                in_=h3g[:, g, :, :].rearrange("p b u -> p (b u)").bitcast(BF16),
+            )
+
+        browf = const.tile([P, P], F32, name="browf")
+        nc.vector.tensor_copy(out=browf[:], in_=brow[:])
+        pb = psa.tile([P, 512], F32, name="pb", tag="a")
+        nc.tensor.transpose(pb[:, 0:P], browf[:], ident[:])
+        bias = const.tile([P, 32], F32, name="bias")
+        nc.vector.tensor_copy(out=bias[:, 0:20], in_=pb[:, 0:20])
+
+        w4g = {}
+        ps1 = {}
+        h4p = {}
+        h4g = {}
+        h4c = [keep.tile([P, B], U32, name="h4c%d" % c, align_bytes=64) for c in range(NG)]
+        h4s = [keep.tile([P, B], U8, name="h4s%d" % c, align_bytes=64) for c in range(NG)]
+
+        def stage_a(i):
+            g_ = grp.tile([P, KP, 4], BF16, name="wg", tag="g", align_bytes=64)
+            regroup(nc, g_, w4r[i], KP, NV_W)
+            w4g[i] = g_
+
+        def stage_b(i):
+            c2, g = divmod(i, NG)
+            codes = cod4.tile([P, KP], U32, name="w4c", tag="w4c", align_bytes=64)
+            scales = cod4.tile([P, KP], U8, name="w4s", tag="w4s", align_bytes=64)
+            nc.vector.quantize_mx(
+                out=codes[:].bitcast(FP8X4),
+                scales=scales[:],
+                in_=w4g[i][:].rearrange("p c t -> p (c t)"),
+            )
+            for t in range(4):
+                if g == 0:
+                    ps1[t] = psa.tile([P, B], F32, name="ps1", tag="a")
+                nc.tensor.matmul_mx(
+                    out=ps1[t][:],
+                    lhsT=codes[:, t * P : (t + 1) * P].bitcast(FP8X4),
+                    lhsT_scale=scales[:, t * P : (t + 1) * P],
+                    rhs=h3c[:, g, :].bitcast(FP8X4),
+                    rhs_scale=h3s[:, g, :],
+                    start=(g == 0),
+                    stop=(g == NG - 1),
                 )
-            elif kind == "Q3":
-                nc.vector.quantize_mx(
-                    out=h3c[:, a, b_ * 256 : (b_ + 1) * 256].bitcast(FP8X4),
-                    scales=h3s[:, a, b_ * 256 : (b_ + 1) * 256],
-                    in_=h3g[:, a, b_ * 256 : (b_ + 1) * 256, :].rearrange("p b u -> p (b u)").bitcast(BF16),
-                )
-            elif kind == "Rv":
-                part("v", grouped(("g4", a), "wg", grp), live[("w4r", a)], 0, NV_W4[a])
-            elif kind == "Rs":
-                part("s", grouped(("g4", a), "wg", grp), live[("w4r", a)], NV_W4[a], 512)
-            elif kind == "Q":
-                codes = cod4.tile([P, KP], U32, name="w4c", tag="w4c", align_bytes=64)
-                scales = cod4.tile([P, KP], U8, name="w4s", tag="w4s", align_bytes=64)
-                nc.vector.quantize_mx(
-                    out=codes[:].bitcast(FP8X4), scales=scales[:], in_=live[("g4", a)][:].rearrange("p c t -> p (c t)")
-                )
-                live[("c4", a)] = (codes, scales)
-            elif kind == "L1":
-                c2, g = divmod(a, NG)
-                codes, scales = live[("c4", a)]
-                for t in range(4):
-                    if g == 0:
-                        live[("ps1", c2, t)] = psa.tile([P, B], F32, name="ps1", tag="a")
-                    nc.tensor.matmul_mx(
-                        out=live[("ps1", c2, t)][:],
-                        lhsT=codes[:, t * P : (t + 1) * P].bitcast(FP8X4),
-                        lhsT_scale=scales[:, t * P : (t + 1) * P],
-                        rhs=h3c[:, g, :].bitcast(FP8X4),
-                        rhs_scale=h3s[:, g, :],
-                        start=(g == 0),
-                        stop=(g == NG - 1),
-                    )
-            elif kind == "X":
-                if ("h4p", a) not in live:
-                    live[("h4p", a)] = h4pool.tile([P, 4, B], BF16, name="h4p", tag="h4p")
-                col = bias[:, 4 * a + b_ : 4 * a + b_ + 1]
-                if ("X%d%d" % (a, b_)) in ON_VECTOR:
+
+        def stage_c(c2, on_vector):
+            hp = h4pool.tile([P, 4, B], BF16, name="h4p", tag="h4p")
+            for t in range(4):
+                col = bias[:, 4 * c2 + t : 4 * c2 + t + 1]
+                if t in on_vector:
                     nc.vector.tensor_scalar(
-                        out=live[("h4p", a)][:, b_, :], in0=live[("ps1", a, b_)][:],
-                        scalar1=col, scalar2=0.0, op0=ALU.add, op1=ALU.max,
+                        out=hp[:, t, :], in0=ps1[t][:], scalar1=col, scalar2=0.0, op0=ALU.add, op1=ALU.max
                     )
                 else:
-                    nc.scalar.activation(
-                        out=live[("h4p", a)][:, b_, :], in_=live[("ps1", a, b_)][:], func=ACT.Relu, bias=col, scale=1.0
-                    )
-            elif kind == "RHv":
-                part("v", grouped(("gh", a), "h4g", h4pool), live[("h4p", a)], 0, NV_H4[a])
-            elif kind == "RHs":
-                part("s", grouped(("gh", a), "h4g", h4pool), live[("h4p", a)], NV_H4[a], 512)
-            elif kind == "QH":
-                nc.vector.quantize_mx(
-                    out=h4c[a][:].bitcast(FP8X4), scales=h4s[a][:], in_=live[("gh", a)][:].rearrange("p b t -> p (b t)")
+                    nc.scalar.activation(out=hp[:, t, :], in_=ps1[t][:], func=ACT.Relu, bias=col, scale=1.0)
+            h4p[c2] = hp
+
+        def stage_d(c2, nv):
+            hg = h4pool.tile([P, B, 4], BF16, name="h4g", tag="h4g", align_bytes=64)
+            regroup(nc, hg, h4p[c2], B, nv)
+            h4g[c2] = hg
+
+        def stage_e(c2):
+            nc.vector.quantize_mx(
+                out=h4c[c2][:].bitcast(FP8X4),
+                scales=h4s[c2][:],
+                in_=h4g[c2][:].rearrange("p b t -> p (b t)"),
+            )
+
+        for i in range(4 * NG + 1):
+            if i < 4 * NG:
+                stage_a(i)
+                if i + LOOKAHEAD < 4 * NG:
+                    load_w4(i + LOOKAHEAD)
+                if i + LOOKAHEAD == 4 * NG - 1:
+                    load_tail()
+            if i >= 6 and i % 4 == 2:
+                stage_d(i // 4 - 1, B)
+            if i >= 1:
+                stage_b(i - 1)
+                if (i - 1) % 4 == 3:
+                    last = i == 4 * NG
+                    stage_c((i - 1) // 4, (1, 3) if last else ())
+            if i >= 7 and i % 4 == 3:
+                stage_e(i // 4 - 1)
+
+        w5c = keep.tile([P, NG, HALF], U32, name="w5c", align_bytes=64)
+        w5s = keep.tile([P, NG, HALF], U8, name="w5s", align_bytes=64)
+        w5g = {}
+
+        def stage_a5(c):
+            g_ = grp.tile([P, HALF, 4], BF16, name="wg5", tag="g", align_bytes=64)
+            regroup(nc, g_, w5r[c], HALF, NV_W)
+            w5g[c] = g_
+
+        def stage_q5(c):
+            nc.vector.quantize_mx(
+                out=w5c[:, c, :].bitcast(FP8X4),
+                scales=w5s[:, c, :],
+                in_=w5g[c][:].rearrange("p c t -> p (c t)"),
+            )
+
+        stage_a5(0)
+        stage_a5(1)
+        stage_d(3, 320)
+        stage_q5(0)
+        stage_a5(2)
+        stage_e(3)
+        stage_q5(1)
+        stage_a5(3)
+        stage_q5(2)
+        stage_q5(3)
+
+        acc = [psa.tile([P, B], F32, name="acc%d" % jt, tag="a") for jt in range(4)]
+        for c in range(NG):
+            for jt in range(4):
+                nc.tensor.matmul_mx(
+                    out=acc[jt][:],
+                    lhsT=w5c[:, c, jt * P : (jt + 1) * P].bitcast(FP8X4),
+                    lhsT_scale=w5s[:, c, jt * P : (jt + 1) * P],
+                    rhs=h4c[c][:].bitcast(FP8X4),
+                    rhs_scale=h4s[c][:],
+                    start=(c == 0),
+                    stop=(c == NG - 1),
                 )
-            elif kind == "R5v":
-                part("v", grouped(("g5", a), "wg", grp), w5r[a], 0, NV_W5[a])
-            elif kind == "R5s":
-                part("s", grouped(("g5", a), "wg", grp), w5r[a], NV_W5[a], 512)
-            elif kind == "Q5":
-                nc.vector.quantize_mx(
-                    out=w5c[:, a, :].bitcast(FP8X4), scales=w5s[:, a, :], in_=live[("g5", a)][:].rearrange("p c t -> p (c t)")
-                )
-            elif kind == "L2":
-                first = "acc" not in live
-                if first:
-                    live["acc"] = [psa.tile([P, B], F32, name="acc%d" % jt, tag="a") for jt in range(4)]
-                    live["nl2"] = 0
-                live["nl2"] += 1
-                for jt in range(4):
-                    nc.tensor.matmul_mx(
-                        out=live["acc"][jt][:],
-                        lhsT=w5c[:, a, jt * P : (jt + 1) * P].bitcast(FP8X4),
-                        lhsT_scale=w5s[:, a, jt * P : (jt + 1) * P],
-                        rhs=h4c[a][:].bitcast(FP8X4),
-                        rhs_scale=h4s[a][:],
-                        start=first,
-                        stop=(live["nl2"] == NG),
-                    )
-            elif kind == "Z":
-                col = bias[:, 16 + a : 17 + a]
-                if ("Z%d" % a) in ON_VECTOR:
-                    nc.vector.tensor_scalar(out=zt[a][:], in0=live["acc"][a][:], scalar1=col, scalar2=None, op0=ALU.add)
-                else:
-                    nc.scalar.activation(out=zt[a][:], in_=live["acc"][a][:], func=ACT.Identity, bias=col, scale=1.0)
-            elif kind == "XM":
-                ch, bt = divmod(a, NBT)
+
+        zt = []
+        for jt in range(4):
+            z = keep.tile([P, B], F32, name="zt%d" % jt)
+            col = bias[:, 16 + jt : 17 + jt]
+            if jt % 2 == 0:
+                nc.scalar.activation(out=z[:], in_=acc[jt][:], func=ACT.Identity, bias=col, scale=1.0)
+            else:
+                nc.vector.tensor_scalar(out=z[:], in0=acc[jt][:], scalar1=col, scalar2=None, op0=ALU.add)
+            zt.append(z)
+        n_exit = 0
+        for ch in range(2):
+            for bt in range(NBT):
                 f = psa.tile([P, 2, 256], F32, name="f", tag="a")
                 nc.tensor.matmul(
-                    out=f[:], lhsT=identb[:],
+                    out=f[:],
+                    lhsT=identb[:],
                     rhs=xr[bt][:, ch * 512 : (ch + 1) * 512].rearrange("p (j e) -> p e j", e=2),
-                    start=True, stop=False,
+                    start=True,
+                    stop=False,
                 )
-                live[("f", a)] = f
-            elif kind == "TF":
-                ch, bt = divmod(a, NBT)
                 for r in range(2):
                     nc.tensor.matmul(
-                        out=live[("f", a)][:, 0, r * P : (r + 1) * P],
+                        out=f[:, 0, r * P : (r + 1) * P],
                         lhsT=zt[2 * ch + r][:, bt * P : (bt + 1) * P],
-                        rhs=ident[:], is_transpose=True, start=False, stop=(r == 1),
+                        rhs=ident[:],
+                        is_transpose=True,
+                        start=False,
+                        stop=(r == 1),
                     )
-            elif kind == "F":
-                ch, bt = divmod(a, NBT)
                 o = opool.tile([P, 256, 2], F32, name="o", tag="o")
-                leave("F%d" % a, o[:], live[("f", a)][:].rearrange("p e j -> p j e"))
+                if n_exit % 2 == 0:
+                    nc.scalar.copy(out=o[:], in_=f[:].rearrange("p e j -> p j e"))
+                else:
+                    nc.vector.tensor_copy(out=o[:], in_=f[:].rearrange("p e j -> p j e"))
+                n_exit += 1
                 nc.sync.dma_start(
-                    out=out[bt * P : (bt + 1) * P, ch * 512 : (ch + 1) * 512], in_=o[:].rearrange("p j e -> p (j e)")
+                    out=out[bt * P : (bt + 1) * P, ch * 512 : (ch + 1) * 512],
+                    in_=o[:].rearrange("p j e -> p (j e)"),
                 )
-            else:
-                assert False, kind
-
-        for op in ORDER:
-            run(op)

@@ -21,20 +21,12 @@ NBT = B // P
 
 FLOPS = 2 * B * MID * MID + 2 * B * MID * HALF
 
-LOOKAHEAD = 12
-NV_W = 264
-
-
-def regroup(nc, dst, src, width, nv):
-    nc.vector.tensor_copy(
-        out=dst[:, 0:nv, :].rearrange("p (c i) t -> p c t i", i=4),
-        in_=src[:, :, 0:nv].rearrange("p t (c i) -> p c t i", i=4),
-    )
-    if nv < width:
-        nc.scalar.copy(
-            out=dst[:, nv:width, :].rearrange("p (c i) t -> p c t i", i=4),
-            in_=src[:, :, nv:width].rearrange("p t (c i) -> p c t i", i=4),
-        )
+LOOKAHEAD = 6
+NV_W4 = [264,264,264,264,264,264,264,264,264,264,264,264,264,264,264,264]
+NV_H4 = [512,512,512,320]
+NV_W5 = [264,264,264,264]
+ON_VECTOR = ["XH01","XH11","XH21","XH31","X31","X33","Z1","Z3","F1","F3","F5","F7"]
+ORDER = [["Db"],["Dh3",0],["Dh3",1],["Dh3",2],["Dh3",3],["DW4",0,0],["DW4",0,1],["DW4",0,2],["DW4",0,3],["DW4",1,0],["DW4",1,1],["TB0"],["TH",0,0],["TH",0,1],["XH",0,0],["XH",0,1],["TH",1,0],["TH",1,1],["XH",1,0],["XH",1,1],["Q3",0,0],["Q3",1,0],["Q3",2,0],["Q3",3,0],["TH",2,0],["TH",2,1],["XH",2,0],["XH",2,1],["TH",3,0],["TH",3,1],["XH",3,0],["XH",3,1],["Q3",0,1],["Q3",1,1],["Q3",2,1],["Q3",3,1],["TB1"],["TB2"],["Rv",0],["Rs",0],["Rv",4],["Rs",4],["DW4",1,2],["Q",0],["L1",0],["Rv",1],["Rs",1],["Q",4],["L1",4],["Rv",5],["Rs",5],["DW4",1,3],["DW5",0],["DW5",1],["DW5",2],["DW5",3],["Dx",0],["Dx",1],["Dx",2],["Dx",3],["Q",1],["L1",1],["Rv",2],["Rs",2],["Q",5],["L1",5],["Rv",6],["Rs",6],["Q",2],["L1",2],["Rv",3],["Rs",3],["Q",6],["L1",6],["Rv",7],["Rs",7],["Q",3],["L1",3],["X",0,0],["X",0,1],["X",0,2],["X",0,3],["Rv",8],["Rs",8],["Q",7],["L1",7],["X",1,0],["X",1,1],["X",1,2],["X",1,3],["Rv",12],["Rs",12],["RHv",0],["Q",8],["L1",8],["Rv",9],["Rs",9],["RHv",1],["Q",12],["L1",12],["QH",0],["Rv",13],["Rs",13],["Q",9],["L1",9],["QH",1],["Rv",10],["Rs",10],["Q",13],["L1",13],["Rv",14],["Rs",14],["Q",10],["L1",10],["Rv",11],["Rs",11],["Q",14],["L1",14],["Rv",15],["Rs",15],["Q",11],["L1",11],["X",2,0],["X",2,1],["X",2,2],["X",2,3],["Q",15],["L1",15],["R5v",0],["R5s",0],["X",3,0],["X",3,1],["X",3,2],["X",3,3],["RHv",2],["R5v",1],["R5s",1],["QH",2],["Q5",0],["RHv",3],["RHs",3],["R5v",2],["R5s",2],["QH",3],["Q5",1],["R5v",3],["R5s",3],["Q5",2],["Q5",3],["L2",0],["L2",1],["L2",2],["L2",3],["XM",0],["XM",1],["XM",2],["XM",3],["Z",0],["Z",1],["Z",2],["Z",3],["TF",0],["F",0],["TF",1],["F",1],["TF",2],["F",2],["TF",3],["F",3],["XM",4],["TF",4],["F",4],["XM",5],["TF",5],["F",5],["XM",6],["TF",6],["F",6],["XM",7],["TF",7],["F",7]]
 
 
 def tile_additivecoupling_pa_kernel(tc, x, h3, W4, b4, W5, b5, out):
@@ -44,242 +36,205 @@ def tile_additivecoupling_pa_kernel(tc, x, h3, W4, b4, W5, b5, out):
         keep = ctx.enter_context(tc.tile_pool(name="keep", bufs=1))
         raw4 = ctx.enter_context(tc.tile_pool(name="raw4", bufs=LOOKAHEAD))
         grp = ctx.enter_context(tc.tile_pool(name="grp", bufs=4))
-        cod4 = ctx.enter_context(tc.tile_pool(name="cod4", bufs=6))
+        cod4 = ctx.enter_context(tc.tile_pool(name="cod4", bufs=8))
         h4pool = ctx.enter_context(tc.tile_pool(name="h4pool", bufs=2))
-        opool = ctx.enter_context(tc.tile_pool(name="opool", bufs=8))
+        opool = ctx.enter_context(tc.tile_pool(name="opool", bufs=4))
         psa = ctx.enter_context(tc.psum_pool(name="psa", bufs=8))
 
+        brow = const.tile([P, P], BF16, name="brow")
+        nc.vector.memset(brow[:], 0.0)
         ident = const.tile([P, P], F32, name="ident")
         make_identity(nc, ident[:])
         identb = const.tile([P, P], BF16, name="identb")
         nc.vector.tensor_copy(out=identb[:], in_=ident[:])
+        browf = const.tile([P, P], F32, name="browf")
+        bias = const.tile([P, 32], F32, name="bias")
 
-        brow = const.tile([P, P], BF16, name="brow")
-        nc.vector.memset(brow[:], 0.0)
-        nc.sync.dma_start(out=brow[0:16, :], in_=b4.rearrange("(r c) -> r c", c=P))
-        nc.sync.dma_start(out=brow[16:20, :], in_=b5.rearrange("(r c) -> r c", c=P))
-
-        h3r = []
-        for bt in range(NBT):
-            t_ = keep.tile([P, MID], BF16, name="h3r%d" % bt)
-            nc.sync.dma_start(out=t_[:], in_=h3[bt * P : (bt + 1) * P, :])
-            h3r.append(t_)
-
-        w4r = {}
-
-        def load_w4(i):
-            c2, g = divmod(i, NG)
-            r = raw4.tile([P, 4, KP], BF16, name="w4r", tag="w4r")
-            for u in range(2):
-                k0 = g * KP + u * 256
-                nc.sync.dma_start(
-                    out=r[:, 2 * u : 2 * u + 2, :],
-                    in_=W4[k0 : k0 + 256, c2 * KP : (c2 + 1) * KP].rearrange("(q e) c -> q e c", e=2),
-                )
-            w4r[i] = r
-
-        for i in range(LOOKAHEAD):
-            load_w4(i)
-
-        w5r = []
-        xr = []
-
-        def load_tail():
-            for c in range(NG):
-                t_ = keep.tile([P, 4, HALF], BF16, name="w5r%d" % c)
-                nc.sync.dma_start(
-                    out=t_[:], in_=W5[c * KP : (c + 1) * KP, :].rearrange("(t p) j -> p t j", p=P)
-                )
-                w5r.append(t_)
-            for bt in range(NBT):
-                t_ = keep.tile([P, 2 * HALF], BF16, name="xr%d" % bt)
-                nc.sync.dma_start(out=t_[:], in_=x[bt * P : (bt + 1) * P, :])
-                xr.append(t_)
-
+        h3r = [keep.tile([P, MID], BF16, name="h3r%d" % bt) for bt in range(NBT)]
+        w5r = [keep.tile([P, 4, HALF], BF16, name="w5r%d" % c) for c in range(NG)]
+        xr = [keep.tile([P, 2 * HALF], BF16, name="xr%d" % bt) for bt in range(NBT)]
         h3g = keep.tile([P, NG, B, 2], F32, name="h3g", align_bytes=64)
         h3c = keep.tile([P, NG, B], U32, name="h3c", align_bytes=64)
         h3s = keep.tile([P, NG, B], U8, name="h3s", align_bytes=64)
-        n_exit = 0
-        for bt in range(NBT):
-            words = h3r[bt][:].bitcast(F32)
-            for gp in range(2):
-                pt = psa.tile([P, 2, 2, P], F32, name="pt", tag="a")
-                for gg in range(2):
-                    for u in range(2):
-                        w0 = (2 * gp + gg) * 256 + u * P
-                        nc.tensor.transpose(pt[:, gg, u, :], words[:, w0 : w0 + P], ident[:])
-                dst = h3g[:, 2 * gp : 2 * gp + 2, bt * P : (bt + 1) * P, :]
-                src = pt[:].rearrange("p g u b -> p g b u")
-                if n_exit % 2 == 0:
-                    nc.scalar.copy(out=dst, in_=src)
-                else:
-                    nc.vector.tensor_copy(out=dst, in_=src)
-                n_exit += 1
-        for g in range(NG):
-            nc.vector.quantize_mx(
-                out=h3c[:, g, :].bitcast(FP8X4),
-                scales=h3s[:, g, :],
-                in_=h3g[:, g, :, :].rearrange("p b u -> p (b u)").bitcast(BF16),
-            )
-
-        browf = const.tile([P, P], F32, name="browf")
-        nc.vector.tensor_copy(out=browf[:], in_=brow[:])
-        pb = psa.tile([P, 512], F32, name="pb", tag="a")
-        nc.tensor.transpose(pb[:, 0:P], browf[:], ident[:])
-        bias = const.tile([P, 32], F32, name="bias")
-        nc.vector.tensor_copy(out=bias[:, 0:20], in_=pb[:, 0:20])
-
-        w4g = {}
-        ps1 = {}
-        h4p = {}
-        h4g = {}
         h4c = [keep.tile([P, B], U32, name="h4c%d" % c, align_bytes=64) for c in range(NG)]
         h4s = [keep.tile([P, B], U8, name="h4s%d" % c, align_bytes=64) for c in range(NG)]
-
-        def stage_a(i):
-            g_ = grp.tile([P, KP, 4], BF16, name="wg", tag="g", align_bytes=64)
-            regroup(nc, g_, w4r[i], KP, NV_W)
-            w4g[i] = g_
-
-        def stage_b(i):
-            c2, g = divmod(i, NG)
-            codes = cod4.tile([P, KP], U32, name="w4c", tag="w4c", align_bytes=64)
-            scales = cod4.tile([P, KP], U8, name="w4s", tag="w4s", align_bytes=64)
-            nc.vector.quantize_mx(
-                out=codes[:].bitcast(FP8X4),
-                scales=scales[:],
-                in_=w4g[i][:].rearrange("p c t -> p (c t)"),
-            )
-            for t in range(4):
-                if g == 0:
-                    ps1[t] = psa.tile([P, B], F32, name="ps1", tag="a")
-                nc.tensor.matmul_mx(
-                    out=ps1[t][:],
-                    lhsT=codes[:, t * P : (t + 1) * P].bitcast(FP8X4),
-                    lhsT_scale=scales[:, t * P : (t + 1) * P],
-                    rhs=h3c[:, g, :].bitcast(FP8X4),
-                    rhs_scale=h3s[:, g, :],
-                    start=(g == 0),
-                    stop=(g == NG - 1),
-                )
-
-        def stage_c(c2, on_vector):
-            hp = h4pool.tile([P, 4, B], BF16, name="h4p", tag="h4p")
-            for t in range(4):
-                col = bias[:, 4 * c2 + t : 4 * c2 + t + 1]
-                if t in on_vector:
-                    nc.vector.tensor_scalar(
-                        out=hp[:, t, :], in0=ps1[t][:], scalar1=col, scalar2=0.0, op0=ALU.add, op1=ALU.max
-                    )
-                else:
-                    nc.scalar.activation(out=hp[:, t, :], in_=ps1[t][:], func=ACT.Relu, bias=col, scale=1.0)
-            h4p[c2] = hp
-
-        def stage_d(c2, nv):
-            hg = h4pool.tile([P, B, 4], BF16, name="h4g", tag="h4g", align_bytes=64)
-            regroup(nc, hg, h4p[c2], B, nv)
-            h4g[c2] = hg
-
-        def stage_e(c2):
-            nc.vector.quantize_mx(
-                out=h4c[c2][:].bitcast(FP8X4),
-                scales=h4s[c2][:],
-                in_=h4g[c2][:].rearrange("p b t -> p (b t)"),
-            )
-
-        for i in range(4 * NG + 1):
-            if i < 4 * NG:
-                stage_a(i)
-                if i + LOOKAHEAD < 4 * NG:
-                    load_w4(i + LOOKAHEAD)
-                if i + LOOKAHEAD == 4 * NG - 1:
-                    load_tail()
-            if i >= 6 and i % 4 == 2:
-                stage_d(i // 4 - 1, B)
-            if i >= 1:
-                stage_b(i - 1)
-                if (i - 1) % 4 == 3:
-                    last = i == 4 * NG
-                    stage_c((i - 1) // 4, (1, 3) if last else ())
-            if i >= 7 and i % 4 == 3:
-                stage_e(i // 4 - 1)
-
         w5c = keep.tile([P, NG, HALF], U32, name="w5c", align_bytes=64)
         w5s = keep.tile([P, NG, HALF], U8, name="w5s", align_bytes=64)
-        w5g = {}
+        zt = [keep.tile([P, B], F32, name="zt%d" % jt) for jt in range(4)]
+        live = {}
 
-        def stage_a5(c):
-            g_ = grp.tile([P, HALF, 4], BF16, name="wg5", tag="g", align_bytes=64)
-            regroup(nc, g_, w5r[c], HALF, NV_W)
-            w5g[c] = g_
-
-        def stage_q5(c):
-            nc.vector.quantize_mx(
-                out=w5c[:, c, :].bitcast(FP8X4),
-                scales=w5s[:, c, :],
-                in_=w5g[c][:].rearrange("p c t -> p (c t)"),
-            )
-
-        stage_a5(0)
-        stage_a5(1)
-        stage_d(3, 320)
-        stage_q5(0)
-        stage_a5(2)
-        stage_e(3)
-        stage_q5(1)
-        stage_a5(3)
-        stage_q5(2)
-        stage_q5(3)
-
-        acc = [psa.tile([P, B], F32, name="acc%d" % jt, tag="a") for jt in range(4)]
-        for c in range(NG):
-            for jt in range(4):
-                nc.tensor.matmul_mx(
-                    out=acc[jt][:],
-                    lhsT=w5c[:, c, jt * P : (jt + 1) * P].bitcast(FP8X4),
-                    lhsT_scale=w5s[:, c, jt * P : (jt + 1) * P],
-                    rhs=h4c[c][:].bitcast(FP8X4),
-                    rhs_scale=h4s[c][:],
-                    start=(c == 0),
-                    stop=(c == NG - 1),
-                )
-
-        zt = []
-        for jt in range(4):
-            z = keep.tile([P, B], F32, name="zt%d" % jt)
-            col = bias[:, 16 + jt : 17 + jt]
-            if jt % 2 == 0:
-                nc.scalar.activation(out=z[:], in_=acc[jt][:], func=ACT.Identity, bias=col, scale=1.0)
+        def part(eng, dst, src, lo, hi):
+            o_ = dst[:, lo:hi, :].rearrange("p (c i) t -> p c t i", i=4)
+            i_ = src[:, :, lo:hi].rearrange("p t (c i) -> p c t i", i=4)
+            if eng == "v":
+                nc.vector.tensor_copy(out=o_, in_=i_)
             else:
-                nc.vector.tensor_scalar(out=z[:], in0=acc[jt][:], scalar1=col, scalar2=None, op0=ALU.add)
-            zt.append(z)
-        n_exit = 0
-        for ch in range(2):
-            for bt in range(NBT):
+                nc.scalar.copy(out=o_, in_=i_)
+
+        def grouped(key, tag, pool):
+            if key not in live:
+                live[key] = pool.tile([P, 512, 4], BF16, name=tag, tag=tag, align_bytes=64)
+            return live[key]
+
+        def leave(name, out_ap, in_ap):
+            if name in ON_VECTOR:
+                nc.vector.tensor_copy(out=out_ap, in_=in_ap)
+            else:
+                nc.scalar.copy(out=out_ap, in_=in_ap)
+
+        def run(op):
+            kind = op[0]
+            a = op[1] if len(op) > 1 else 0
+            b_ = op[2] if len(op) > 2 else 0
+            if kind == "Db":
+                nc.sync.dma_start(out=brow[0:16, :], in_=b4.rearrange("(r c) -> r c", c=P))
+                nc.sync.dma_start(out=brow[16:20, :], in_=b5.rearrange("(r c) -> r c", c=P))
+            elif kind == "Dh3":
+                nc.sync.dma_start(out=h3r[a][:], in_=h3[a * P : (a + 1) * P, :])
+            elif kind == "DW4":
+                r = raw4.tile([P, 4, 2 * KP], BF16, name="w4r", tag="w4r")
+                for u in range(2):
+                    k0 = b_ * KP + u * 256
+                    nc.sync.dma_start(
+                        out=r[:, 2 * u : 2 * u + 2, :],
+                        in_=W4[k0 : k0 + 256, a * 2 * KP : (a + 1) * 2 * KP].rearrange("(q e) c -> q e c", e=2),
+                    )
+                for s_ in range(2):
+                    live[("w4r", (2 * a + s_) * NG + b_)] = r[:, :, s_ * KP : (s_ + 1) * KP]
+            elif kind == "DW5":
+                nc.sync.dma_start(out=w5r[a][:], in_=W5[a * KP : (a + 1) * KP, :].rearrange("(t p) j -> p t j", p=P))
+            elif kind == "Dx":
+                nc.sync.dma_start(out=xr[a][:], in_=x[a * P : (a + 1) * P, :])
+            elif kind == "TB0":
+                nc.vector.tensor_copy(out=browf[:], in_=brow[:])
+            elif kind == "TB1":
+                live["pb"] = psa.tile([P, 512], F32, name="pb", tag="a")
+                nc.tensor.transpose(live["pb"][:, 0:P], browf[:], ident[:])
+            elif kind == "TB2":
+                nc.vector.tensor_copy(out=bias[:, 0:20], in_=live["pb"][:, 0:20])
+            elif kind == "TH":
+                pt = psa.tile([P, 2, 2, P], F32, name="pt", tag="a")
+                words = h3r[a][:].bitcast(F32)
+                for gg in range(2):
+                    for u in range(2):
+                        w0 = (2 * b_ + gg) * 256 + u * P
+                        nc.tensor.transpose(pt[:, gg, u, :], words[:, w0 : w0 + P], ident[:])
+                live[("pt", a, b_)] = pt
+            elif kind == "XH":
+                leave(
+                    "XH%d%d" % (a, b_),
+                    h3g[:, 2 * b_ : 2 * b_ + 2, a * P : (a + 1) * P, :],
+                    live[("pt", a, b_)][:].rearrange("p g u b -> p g b u"),
+                )
+            elif kind == "Q3":
+                nc.vector.quantize_mx(
+                    out=h3c[:, a, b_ * 256 : (b_ + 1) * 256].bitcast(FP8X4),
+                    scales=h3s[:, a, b_ * 256 : (b_ + 1) * 256],
+                    in_=h3g[:, a, b_ * 256 : (b_ + 1) * 256, :].rearrange("p b u -> p (b u)").bitcast(BF16),
+                )
+            elif kind == "Rv":
+                part("v", grouped(("g4", a), "wg", grp), live[("w4r", a)], 0, NV_W4[a])
+            elif kind == "Rs":
+                part("s", grouped(("g4", a), "wg", grp), live[("w4r", a)], NV_W4[a], 512)
+            elif kind == "Q":
+                codes = cod4.tile([P, KP], U32, name="w4c", tag="w4c", align_bytes=64)
+                scales = cod4.tile([P, KP], U8, name="w4s", tag="w4s", align_bytes=64)
+                nc.vector.quantize_mx(
+                    out=codes[:].bitcast(FP8X4), scales=scales[:], in_=live[("g4", a)][:].rearrange("p c t -> p (c t)")
+                )
+                live[("c4", a)] = (codes, scales)
+            elif kind == "L1":
+                c2, g = divmod(a, NG)
+                codes, scales = live[("c4", a)]
+                for t in range(4):
+                    if g == 0:
+                        live[("ps1", c2, t)] = psa.tile([P, B], F32, name="ps1", tag="a")
+                    nc.tensor.matmul_mx(
+                        out=live[("ps1", c2, t)][:],
+                        lhsT=codes[:, t * P : (t + 1) * P].bitcast(FP8X4),
+                        lhsT_scale=scales[:, t * P : (t + 1) * P],
+                        rhs=h3c[:, g, :].bitcast(FP8X4),
+                        rhs_scale=h3s[:, g, :],
+                        start=(g == 0),
+                        stop=(g == NG - 1),
+                    )
+            elif kind == "X":
+                if ("h4p", a) not in live:
+                    live[("h4p", a)] = h4pool.tile([P, 4, B], BF16, name="h4p", tag="h4p")
+                col = bias[:, 4 * a + b_ : 4 * a + b_ + 1]
+                if ("X%d%d" % (a, b_)) in ON_VECTOR:
+                    nc.vector.tensor_scalar(
+                        out=live[("h4p", a)][:, b_, :], in0=live[("ps1", a, b_)][:],
+                        scalar1=col, scalar2=0.0, op0=ALU.add, op1=ALU.max,
+                    )
+                else:
+                    nc.scalar.activation(
+                        out=live[("h4p", a)][:, b_, :], in_=live[("ps1", a, b_)][:], func=ACT.Relu, bias=col, scale=1.0
+                    )
+            elif kind == "RHv":
+                part("v", grouped(("gh", a), "h4g", h4pool), live[("h4p", a)], 0, NV_H4[a])
+            elif kind == "RHs":
+                part("s", grouped(("gh", a), "h4g", h4pool), live[("h4p", a)], NV_H4[a], 512)
+            elif kind == "QH":
+                nc.vector.quantize_mx(
+                    out=h4c[a][:].bitcast(FP8X4), scales=h4s[a][:], in_=live[("gh", a)][:].rearrange("p b t -> p (b t)")
+                )
+            elif kind == "R5v":
+                part("v", grouped(("g5", a), "wg", grp), w5r[a], 0, NV_W5[a])
+            elif kind == "R5s":
+                part("s", grouped(("g5", a), "wg", grp), w5r[a], NV_W5[a], 512)
+            elif kind == "Q5":
+                nc.vector.quantize_mx(
+                    out=w5c[:, a, :].bitcast(FP8X4), scales=w5s[:, a, :], in_=live[("g5", a)][:].rearrange("p c t -> p (c t)")
+                )
+            elif kind == "L2":
+                first = "acc" not in live
+                if first:
+                    live["acc"] = [psa.tile([P, B], F32, name="acc%d" % jt, tag="a") for jt in range(4)]
+                    live["nl2"] = 0
+                live["nl2"] += 1
+                for jt in range(4):
+                    nc.tensor.matmul_mx(
+                        out=live["acc"][jt][:],
+                        lhsT=w5c[:, a, jt * P : (jt + 1) * P].bitcast(FP8X4),
+                        lhsT_scale=w5s[:, a, jt * P : (jt + 1) * P],
+                        rhs=h4c[a][:].bitcast(FP8X4),
+                        rhs_scale=h4s[a][:],
+                        start=first,
+                        stop=(live["nl2"] == NG),
+                    )
+            elif kind == "Z":
+                col = bias[:, 16 + a : 17 + a]
+                if ("Z%d" % a) in ON_VECTOR:
+                    nc.vector.tensor_scalar(out=zt[a][:], in0=live["acc"][a][:], scalar1=col, scalar2=None, op0=ALU.add)
+                else:
+                    nc.scalar.activation(out=zt[a][:], in_=live["acc"][a][:], func=ACT.Identity, bias=col, scale=1.0)
+            elif kind == "XM":
+                ch, bt = divmod(a, NBT)
                 f = psa.tile([P, 2, 256], F32, name="f", tag="a")
                 nc.tensor.matmul(
-                    out=f[:],
-                    lhsT=identb[:],
+                    out=f[:], lhsT=identb[:],
                     rhs=xr[bt][:, ch * 512 : (ch + 1) * 512].rearrange("p (j e) -> p e j", e=2),
-                    start=True,
-                    stop=False,
+                    start=True, stop=False,
                 )
+                live[("f", a)] = f
+            elif kind == "TF":
+                ch, bt = divmod(a, NBT)
                 for r in range(2):
                     nc.tensor.matmul(
-                        out=f[:, 0, r * P : (r + 1) * P],
+                        out=live[("f", a)][:, 0, r * P : (r + 1) * P],
                         lhsT=zt[2 * ch + r][:, bt * P : (bt + 1) * P],
-                        rhs=ident[:],
-                        is_transpose=True,
-                        start=False,
-                        stop=(r == 1),
+                        rhs=ident[:], is_transpose=True, start=False, stop=(r == 1),
                     )
+            elif kind == "F":
+                ch, bt = divmod(a, NBT)
                 o = opool.tile([P, 256, 2], F32, name="o", tag="o")
-                if n_exit % 2 == 0:
-                    nc.scalar.copy(out=o[:], in_=f[:].rearrange("p e j -> p j e"))
-                else:
-                    nc.vector.tensor_copy(out=o[:], in_=f[:].rearrange("p e j -> p j e"))
-                n_exit += 1
+                leave("F%d" % a, o[:], live[("f", a)][:].rearrange("p e j -> p j e"))
                 nc.sync.dma_start(
-                    out=out[bt * P : (bt + 1) * P, ch * 512 : (ch + 1) * 512],
-                    in_=o[:].rearrange("p j e -> p (j e)"),
+                    out=out[bt * P : (bt + 1) * P, ch * 512 : (ch + 1) * 512], in_=o[:].rearrange("p j e -> p (j e)")
                 )
+            else:
+                assert False, kind
+
+        for op in ORDER:
+            run(op)

@@ -21,12 +21,20 @@ NBT = B // P
 
 FLOPS = 2 * B * MID * MID + 2 * B * MID * HALF
 
-LOOKAHEAD = 6
-NV_W4 = [264,264,264,264,264,264,264,264,264,264,264,264,264,264,264,264]
-NV_H4 = [512,512,512,320]
-NV_W5 = [264,264,264,264]
-ON_VECTOR = ["XH01","XH11","XH21","XH31","X31","X33","Z1","Z3","F1","F3","F5","F7"]
-ORDER = [["Db"],["Dh3",0],["Dh3",1],["Dh3",2],["Dh3",3],["DW4",0,0],["DW4",0,1],["DW4",0,2],["DW4",0,3],["DW4",1,0],["DW4",1,1],["TB0"],["TH",0,0],["TH",0,1],["XH",0,0],["XH",0,1],["TH",1,0],["TH",1,1],["XH",1,0],["XH",1,1],["Q3",0,0],["Q3",1,0],["Q3",2,0],["Q3",3,0],["TH",2,0],["TH",2,1],["XH",2,0],["XH",2,1],["TH",3,0],["TH",3,1],["XH",3,0],["XH",3,1],["Q3",0,1],["Q3",1,1],["Q3",2,1],["Q3",3,1],["TB1"],["TB2"],["Rv",0],["Rs",0],["Rv",4],["Rs",4],["DW4",1,2],["Q",0],["L1",0],["Rv",1],["Rs",1],["Q",4],["L1",4],["Rv",5],["Rs",5],["DW4",1,3],["DW5",0],["DW5",1],["DW5",2],["DW5",3],["Dx",0],["Dx",1],["Dx",2],["Dx",3],["Q",1],["L1",1],["Rv",2],["Rs",2],["Q",5],["L1",5],["Rv",6],["Rs",6],["Q",2],["L1",2],["Rv",3],["Rs",3],["Q",6],["L1",6],["Rv",7],["Rs",7],["Q",3],["L1",3],["X",0,0],["X",0,1],["X",0,2],["X",0,3],["Rv",8],["Rs",8],["Q",7],["L1",7],["X",1,0],["X",1,1],["X",1,2],["X",1,3],["Rv",12],["Rs",12],["RHv",0],["Q",8],["L1",8],["Rv",9],["Rs",9],["RHv",1],["Q",12],["L1",12],["QH",0],["Rv",13],["Rs",13],["Q",9],["L1",9],["QH",1],["Rv",10],["Rs",10],["Q",13],["L1",13],["Rv",14],["Rs",14],["Q",10],["L1",10],["Rv",11],["Rs",11],["Q",14],["L1",14],["Rv",15],["Rs",15],["Q",11],["L1",11],["X",2,0],["X",2,1],["X",2,2],["X",2,3],["Q",15],["L1",15],["R5v",0],["R5s",0],["X",3,0],["X",3,1],["X",3,2],["X",3,3],["RHv",2],["R5v",1],["R5s",1],["QH",2],["Q5",0],["RHv",3],["RHs",3],["R5v",2],["R5s",2],["QH",3],["Q5",1],["R5v",3],["R5s",3],["Q5",2],["Q5",3],["L2",0],["L2",1],["L2",2],["L2",3],["XM",0],["XM",1],["XM",2],["XM",3],["Z",0],["Z",1],["Z",2],["Z",3],["TF",0],["F",0],["TF",1],["F",1],["TF",2],["F",2],["TF",3],["F",3],["XM",4],["TF",4],["F",4],["XM",5],["TF",5],["F",5],["XM",6],["TF",6],["F",6],["XM",7],["TF",7],["F",7]]
+LOOKAHEAD = 12
+NV_W = 264
+
+
+def regroup(nc, dst, src, width, nv):
+    nc.vector.tensor_copy(
+        out=dst[:, 0:nv, :].rearrange("p (c i) t -> p c t i", i=4),
+        in_=src[:, :, 0:nv].rearrange("p t (c i) -> p c t i", i=4),
+    )
+    if nv < width:
+        nc.scalar.copy(
+            out=dst[:, nv:width, :].rearrange("p (c i) t -> p c t i", i=4),
+            in_=src[:, :, nv:width].rearrange("p t (c i) -> p c t i", i=4),
+        )
 
 
 def tile_additivecoupling_pa_kernel(tc, x, h3, W4, b4, W5, b5, out):
@@ -36,205 +44,239 @@ def tile_additivecoupling_pa_kernel(tc, x, h3, W4, b4, W5, b5, out):
         keep = ctx.enter_context(tc.tile_pool(name="keep", bufs=1))
         raw4 = ctx.enter_context(tc.tile_pool(name="raw4", bufs=LOOKAHEAD))
         grp = ctx.enter_context(tc.tile_pool(name="grp", bufs=4))
-        cod4 = ctx.enter_context(tc.tile_pool(name="cod4", bufs=8))
+        cod4 = ctx.enter_context(tc.tile_pool(name="cod4", bufs=6))
         h4pool = ctx.enter_context(tc.tile_pool(name="h4pool", bufs=2))
-        opool = ctx.enter_context(tc.tile_pool(name="opool", bufs=4))
+        opool = ctx.enter_context(tc.tile_pool(name="opool", bufs=8))
         psa = ctx.enter_context(tc.psum_pool(name="psa", bufs=8))
 
-        brow = const.tile([P, P], BF16, name="brow")
-        nc.vector.memset(brow[:], 0.0)
         ident = const.tile([P, P], F32, name="ident")
         make_identity(nc, ident[:])
         identb = const.tile([P, P], BF16, name="identb")
         nc.vector.tensor_copy(out=identb[:], in_=ident[:])
-        browf = const.tile([P, P], F32, name="browf")
-        bias = const.tile([P, 32], F32, name="bias")
 
-        h3r = [keep.tile([P, MID], BF16, name="h3r%d" % bt) for bt in range(NBT)]
-        w5r = [keep.tile([P, 4, HALF], BF16, name="w5r%d" % c) for c in range(NG)]
-        xr = [keep.tile([P, 2 * HALF], BF16, name="xr%d" % bt) for bt in range(NBT)]
+        brow = const.tile([P, P], BF16, name="brow")
+        nc.vector.memset(brow[:], 0.0)
+        nc.sync.dma_start(out=brow[0:16, :], in_=b4.rearrange("(r c) -> r c", c=P))
+        nc.sync.dma_start(out=brow[16:20, :], in_=b5.rearrange("(r c) -> r c", c=P))
+
+        h3r = []
+        for bt in range(NBT):
+            t_ = keep.tile([P, MID], BF16, name="h3r%d" % bt)
+            nc.sync.dma_start(out=t_[:], in_=h3[bt * P : (bt + 1) * P, :])
+            h3r.append(t_)
+
+        w4r = {}
+
+        def load_w4(i):
+            c2, g = divmod(i, NG)
+            r = raw4.tile([P, 4, KP], BF16, name="w4r", tag="w4r")
+            nc.sync.dma_start(
+                out=r[:],
+                in_=W4[g * KP : (g + 1) * KP, c2 * KP : (c2 + 1) * KP].rearrange("(p j) c -> p j c", j=4),
+            )
+            w4r[i] = r
+
+        for i in range(LOOKAHEAD):
+            load_w4(i)
+
+        w5r = []
+        xr = []
+
+        def load_tail():
+            for c in range(NG):
+                t_ = keep.tile([P, 4, HALF], BF16, name="w5r%d" % c)
+                nc.sync.dma_start(
+                    out=t_[:], in_=W5[c * KP : (c + 1) * KP, :].rearrange("(t p) j -> p t j", p=P)
+                )
+                w5r.append(t_)
+            xall = keep.tile([P, NBT, 2 * HALF], BF16, name="xall")
+            nc.sync.dma_start(out=xall[:], in_=x.rearrange("(bt p) c -> p bt c", p=P))
+            for bt in range(NBT):
+                xr.append(xall[:, bt, :])
+
         h3g = keep.tile([P, NG, B, 2], F32, name="h3g", align_bytes=64)
         h3c = keep.tile([P, NG, B], U32, name="h3c", align_bytes=64)
         h3s = keep.tile([P, NG, B], U8, name="h3s", align_bytes=64)
-        h4c = [keep.tile([P, B], U32, name="h4c%d" % c, align_bytes=64) for c in range(NG)]
-        h4s = [keep.tile([P, B], U8, name="h4s%d" % c, align_bytes=64) for c in range(NG)]
-        w5c = keep.tile([P, NG, HALF], U32, name="w5c", align_bytes=64)
-        w5s = keep.tile([P, NG, HALF], U8, name="w5s", align_bytes=64)
-        zt = [keep.tile([P, B], F32, name="zt%d" % jt) for jt in range(4)]
-        live = {}
-
-        def part(eng, dst, src, lo, hi):
-            o_ = dst[:, lo:hi, :].rearrange("p (c i) t -> p c t i", i=4)
-            i_ = src[:, :, lo:hi].rearrange("p t (c i) -> p c t i", i=4)
-            if eng == "v":
-                nc.vector.tensor_copy(out=o_, in_=i_)
-            else:
-                nc.scalar.copy(out=o_, in_=i_)
-
-        def grouped(key, tag, pool):
-            if key not in live:
-                live[key] = pool.tile([P, 512, 4], BF16, name=tag, tag=tag, align_bytes=64)
-            return live[key]
-
-        def leave(name, out_ap, in_ap):
-            if name in ON_VECTOR:
-                nc.vector.tensor_copy(out=out_ap, in_=in_ap)
-            else:
-                nc.scalar.copy(out=out_ap, in_=in_ap)
-
-        def run(op):
-            kind = op[0]
-            a = op[1] if len(op) > 1 else 0
-            b_ = op[2] if len(op) > 2 else 0
-            if kind == "Db":
-                nc.sync.dma_start(out=brow[0:16, :], in_=b4.rearrange("(r c) -> r c", c=P))
-                nc.sync.dma_start(out=brow[16:20, :], in_=b5.rearrange("(r c) -> r c", c=P))
-            elif kind == "Dh3":
-                nc.sync.dma_start(out=h3r[a][:], in_=h3[a * P : (a + 1) * P, :])
-            elif kind == "DW4":
-                r = raw4.tile([P, 4, 2 * KP], BF16, name="w4r", tag="w4r")
-                for u in range(2):
-                    k0 = b_ * KP + u * 256
-                    nc.sync.dma_start(
-                        out=r[:, 2 * u : 2 * u + 2, :],
-                        in_=W4[k0 : k0 + 256, a * 2 * KP : (a + 1) * 2 * KP].rearrange("(q e) c -> q e c", e=2),
-                    )
-                for s_ in range(2):
-                    live[("w4r", (2 * a + s_) * NG + b_)] = r[:, :, s_ * KP : (s_ + 1) * KP]
-            elif kind == "DW5":
-                nc.sync.dma_start(out=w5r[a][:], in_=W5[a * KP : (a + 1) * KP, :].rearrange("(t p) j -> p t j", p=P))
-            elif kind == "Dx":
-                nc.sync.dma_start(out=xr[a][:], in_=x[a * P : (a + 1) * P, :])
-            elif kind == "TB0":
-                nc.vector.tensor_copy(out=browf[:], in_=brow[:])
-            elif kind == "TB1":
-                live["pb"] = psa.tile([P, 512], F32, name="pb", tag="a")
-                nc.tensor.transpose(live["pb"][:, 0:P], browf[:], ident[:])
-            elif kind == "TB2":
-                nc.vector.tensor_copy(out=bias[:, 0:20], in_=live["pb"][:, 0:20])
-            elif kind == "TH":
+        n_exit = 0
+        for bt in range(NBT):
+            words = h3r[bt][:].bitcast(F32).rearrange("p (g q u) -> p g u q", g=NG, u=2)
+            for gp in range(2):
                 pt = psa.tile([P, 2, 2, P], F32, name="pt", tag="a")
-                words = h3r[a][:].bitcast(F32)
                 for gg in range(2):
                     for u in range(2):
-                        w0 = (2 * b_ + gg) * 256 + u * P
-                        nc.tensor.transpose(pt[:, gg, u, :], words[:, w0 : w0 + P], ident[:])
-                live[("pt", a, b_)] = pt
-            elif kind == "XH":
-                leave(
-                    "XH%d%d" % (a, b_),
-                    h3g[:, 2 * b_ : 2 * b_ + 2, a * P : (a + 1) * P, :],
-                    live[("pt", a, b_)][:].rearrange("p g u b -> p g b u"),
+                        nc.tensor.transpose(pt[:, gg, u, :], words[:, 2 * gp + gg, u, :], ident[:])
+                dst = h3g[:, 2 * gp : 2 * gp + 2, bt * P : (bt + 1) * P, :]
+                src = pt[:].rearrange("p g u b -> p g b u")
+                if n_exit % 2 == 0:
+                    nc.scalar.copy(out=dst, in_=src)
+                else:
+                    nc.vector.tensor_copy(out=dst, in_=src)
+                n_exit += 1
+        for g in range(NG):
+            nc.vector.quantize_mx(
+                out=h3c[:, g, :].bitcast(FP8X4),
+                scales=h3s[:, g, :],
+                in_=h3g[:, g, :, :].rearrange("p b u -> p (b u)").bitcast(BF16),
+            )
+
+        browf = const.tile([P, P], F32, name="browf")
+        nc.vector.tensor_copy(out=browf[:], in_=brow[:])
+        pb = psa.tile([P, 512], F32, name="pb", tag="a")
+        nc.tensor.transpose(pb[:, 0:P], browf[:], ident[:])
+        bias = const.tile([P, 32], F32, name="bias")
+        nc.vector.tensor_copy(out=bias[:, 0:20], in_=pb[:, 0:20])
+
+        w4g = {}
+        ps1 = {}
+        h4p = {}
+        h4g = {}
+        h4c = [keep.tile([P, B], U32, name="h4c%d" % c, align_bytes=64) for c in range(NG)]
+        h4s = [keep.tile([P, B], U8, name="h4s%d" % c, align_bytes=64) for c in range(NG)]
+
+        def stage_a(i):
+            g_ = grp.tile([P, KP, 4], BF16, name="wg", tag="g", align_bytes=64)
+            regroup(nc, g_, w4r[i], KP, NV_W)
+            w4g[i] = g_
+
+        def stage_b(i):
+            c2, g = divmod(i, NG)
+            codes = cod4.tile([P, KP], U32, name="w4c", tag="w4c", align_bytes=64)
+            scales = cod4.tile([P, KP], U8, name="w4s", tag="w4s", align_bytes=64)
+            nc.vector.quantize_mx(
+                out=codes[:].bitcast(FP8X4),
+                scales=scales[:],
+                in_=w4g[i][:].rearrange("p c t -> p (c t)"),
+            )
+            for t in range(4):
+                if g == 0:
+                    ps1[t] = psa.tile([P, B], F32, name="ps1", tag="a")
+                nc.tensor.matmul_mx(
+                    out=ps1[t][:],
+                    lhsT=codes[:, t * P : (t + 1) * P].bitcast(FP8X4),
+                    lhsT_scale=scales[:, t * P : (t + 1) * P],
+                    rhs=h3c[:, g, :].bitcast(FP8X4),
+                    rhs_scale=h3s[:, g, :],
+                    start=(g == 0),
+                    stop=(g == NG - 1),
                 )
-            elif kind == "Q3":
-                nc.vector.quantize_mx(
-                    out=h3c[:, a, b_ * 256 : (b_ + 1) * 256].bitcast(FP8X4),
-                    scales=h3s[:, a, b_ * 256 : (b_ + 1) * 256],
-                    in_=h3g[:, a, b_ * 256 : (b_ + 1) * 256, :].rearrange("p b u -> p (b u)").bitcast(BF16),
-                )
-            elif kind == "Rv":
-                part("v", grouped(("g4", a), "wg", grp), live[("w4r", a)], 0, NV_W4[a])
-            elif kind == "Rs":
-                part("s", grouped(("g4", a), "wg", grp), live[("w4r", a)], NV_W4[a], 512)
-            elif kind == "Q":
-                codes = cod4.tile([P, KP], U32, name="w4c", tag="w4c", align_bytes=64)
-                scales = cod4.tile([P, KP], U8, name="w4s", tag="w4s", align_bytes=64)
-                nc.vector.quantize_mx(
-                    out=codes[:].bitcast(FP8X4), scales=scales[:], in_=live[("g4", a)][:].rearrange("p c t -> p (c t)")
-                )
-                live[("c4", a)] = (codes, scales)
-            elif kind == "L1":
-                c2, g = divmod(a, NG)
-                codes, scales = live[("c4", a)]
-                for t in range(4):
-                    if g == 0:
-                        live[("ps1", c2, t)] = psa.tile([P, B], F32, name="ps1", tag="a")
-                    nc.tensor.matmul_mx(
-                        out=live[("ps1", c2, t)][:],
-                        lhsT=codes[:, t * P : (t + 1) * P].bitcast(FP8X4),
-                        lhsT_scale=scales[:, t * P : (t + 1) * P],
-                        rhs=h3c[:, g, :].bitcast(FP8X4),
-                        rhs_scale=h3s[:, g, :],
-                        start=(g == 0),
-                        stop=(g == NG - 1),
-                    )
-            elif kind == "X":
-                if ("h4p", a) not in live:
-                    live[("h4p", a)] = h4pool.tile([P, 4, B], BF16, name="h4p", tag="h4p")
-                col = bias[:, 4 * a + b_ : 4 * a + b_ + 1]
-                if ("X%d%d" % (a, b_)) in ON_VECTOR:
+
+        def stage_c(c2, on_vector):
+            hp = h4pool.tile([P, 4, B], BF16, name="h4p", tag="h4p")
+            for t in range(4):
+                col = bias[:, 4 * c2 + t : 4 * c2 + t + 1]
+                if t in on_vector:
                     nc.vector.tensor_scalar(
-                        out=live[("h4p", a)][:, b_, :], in0=live[("ps1", a, b_)][:],
-                        scalar1=col, scalar2=0.0, op0=ALU.add, op1=ALU.max,
+                        out=hp[:, t, :], in0=ps1[t][:], scalar1=col, scalar2=0.0, op0=ALU.add, op1=ALU.max
                     )
                 else:
-                    nc.scalar.activation(
-                        out=live[("h4p", a)][:, b_, :], in_=live[("ps1", a, b_)][:], func=ACT.Relu, bias=col, scale=1.0
-                    )
-            elif kind == "RHv":
-                part("v", grouped(("gh", a), "h4g", h4pool), live[("h4p", a)], 0, NV_H4[a])
-            elif kind == "RHs":
-                part("s", grouped(("gh", a), "h4g", h4pool), live[("h4p", a)], NV_H4[a], 512)
-            elif kind == "QH":
-                nc.vector.quantize_mx(
-                    out=h4c[a][:].bitcast(FP8X4), scales=h4s[a][:], in_=live[("gh", a)][:].rearrange("p b t -> p (b t)")
+                    nc.scalar.activation(out=hp[:, t, :], in_=ps1[t][:], func=ACT.Relu, bias=col, scale=1.0)
+            h4p[c2] = hp
+
+        def stage_d(c2, nv):
+            hg = h4pool.tile([P, B, 4], BF16, name="h4g", tag="h4g", align_bytes=64)
+            regroup(nc, hg, h4p[c2], B, nv)
+            h4g[c2] = hg
+
+        def stage_e(c2):
+            nc.vector.quantize_mx(
+                out=h4c[c2][:].bitcast(FP8X4),
+                scales=h4s[c2][:],
+                in_=h4g[c2][:].rearrange("p b t -> p (b t)"),
+            )
+
+        for i in range(4 * NG + 1):
+            if i < 4 * NG:
+                stage_a(i)
+                if i + LOOKAHEAD < 4 * NG:
+                    load_w4(i + LOOKAHEAD)
+                if i + LOOKAHEAD == 4 * NG - 1:
+                    load_tail()
+            if i >= 6 and i % 4 == 2:
+                stage_d(i // 4 - 1, B)
+            if i >= 1:
+                stage_b(i - 1)
+                if (i - 1) % 4 == 3:
+                    last = i == 4 * NG
+                    stage_c((i - 1) // 4, (1, 3) if last else ())
+            if i >= 7 and i % 4 == 3:
+                stage_e(i // 4 - 1)
+
+        w5c = keep.tile([P, NG, HALF], U32, name="w5c", align_bytes=64)
+        w5s = keep.tile([P, NG, HALF], U8, name="w5s", align_bytes=64)
+        w5g = {}
+
+        def stage_a5(c):
+            g_ = grp.tile([P, HALF, 4], BF16, name="wg5", tag="g", align_bytes=64)
+            regroup(nc, g_, w5r[c], HALF, NV_W)
+            w5g[c] = g_
+
+        def stage_q5(c):
+            nc.vector.quantize_mx(
+                out=w5c[:, c, :].bitcast(FP8X4),
+                scales=w5s[:, c, :],
+                in_=w5g[c][:].rearrange("p c t -> p (c t)"),
+            )
+
+        stage_a5(0)
+        stage_a5(1)
+        stage_d(3, 320)
+        stage_q5(0)
+        stage_a5(2)
+        stage_e(3)
+        stage_q5(1)
+        stage_a5(3)
+        stage_q5(2)
+        stage_q5(3)
+
+        acc = [psa.tile([P, B], F32, name="acc%d" % jt, tag="a") for jt in range(4)]
+        for c in range(NG):
+            for jt in range(4):
+                nc.tensor.matmul_mx(
+                    out=acc[jt][:],
+                    lhsT=w5c[:, c, jt * P : (jt + 1) * P].bitcast(FP8X4),
+                    lhsT_scale=w5s[:, c, jt * P : (jt + 1) * P],
+                    rhs=h4c[c][:].bitcast(FP8X4),
+                    rhs_scale=h4s[c][:],
+                    start=(c == 0),
+                    stop=(c == NG - 1),
                 )
-            elif kind == "R5v":
-                part("v", grouped(("g5", a), "wg", grp), w5r[a], 0, NV_W5[a])
-            elif kind == "R5s":
-                part("s", grouped(("g5", a), "wg", grp), w5r[a], NV_W5[a], 512)
-            elif kind == "Q5":
-                nc.vector.quantize_mx(
-                    out=w5c[:, a, :].bitcast(FP8X4), scales=w5s[:, a, :], in_=live[("g5", a)][:].rearrange("p c t -> p (c t)")
-                )
-            elif kind == "L2":
-                first = "acc" not in live
-                if first:
-                    live["acc"] = [psa.tile([P, B], F32, name="acc%d" % jt, tag="a") for jt in range(4)]
-                    live["nl2"] = 0
-                live["nl2"] += 1
-                for jt in range(4):
-                    nc.tensor.matmul_mx(
-                        out=live["acc"][jt][:],
-                        lhsT=w5c[:, a, jt * P : (jt + 1) * P].bitcast(FP8X4),
-                        lhsT_scale=w5s[:, a, jt * P : (jt + 1) * P],
-                        rhs=h4c[a][:].bitcast(FP8X4),
-                        rhs_scale=h4s[a][:],
-                        start=first,
-                        stop=(live["nl2"] == NG),
-                    )
-            elif kind == "Z":
-                col = bias[:, 16 + a : 17 + a]
-                if ("Z%d" % a) in ON_VECTOR:
-                    nc.vector.tensor_scalar(out=zt[a][:], in0=live["acc"][a][:], scalar1=col, scalar2=None, op0=ALU.add)
-                else:
-                    nc.scalar.activation(out=zt[a][:], in_=live["acc"][a][:], func=ACT.Identity, bias=col, scale=1.0)
-            elif kind == "XM":
-                ch, bt = divmod(a, NBT)
+
+        zt = []
+        for jt in range(4):
+            z = keep.tile([P, B], F32, name="zt%d" % jt)
+            col = bias[:, 16 + jt : 17 + jt]
+            if jt % 2 == 0:
+                nc.scalar.activation(out=z[:], in_=acc[jt][:], func=ACT.Identity, bias=col, scale=1.0)
+            else:
+                nc.vector.tensor_scalar(out=z[:], in0=acc[jt][:], scalar1=col, scalar2=None, op0=ALU.add)
+            zt.append(z)
+        n_exit = 0
+        for ch in range(2):
+            for bt in range(NBT):
                 f = psa.tile([P, 2, 256], F32, name="f", tag="a")
                 nc.tensor.matmul(
-                    out=f[:], lhsT=identb[:],
+                    out=f[:],
+                    lhsT=identb[:],
                     rhs=xr[bt][:, ch * 512 : (ch + 1) * 512].rearrange("p (j e) -> p e j", e=2),
-                    start=True, stop=False,
+                    start=True,
+                    stop=False,
                 )
-                live[("f", a)] = f
-            elif kind == "TF":
-                ch, bt = divmod(a, NBT)
                 for r in range(2):
                     nc.tensor.matmul(
-                        out=live[("f", a)][:, 0, r * P : (r + 1) * P],
+                        out=f[:, 0, r * P : (r + 1) * P],
                         lhsT=zt[2 * ch + r][:, bt * P : (bt + 1) * P],
-                        rhs=ident[:], is_transpose=True, start=False, stop=(r == 1),
+                        rhs=ident[:],
+                        is_transpose=True,
+                        start=False,
+                        stop=(r == 1),
                     )
-            elif kind == "F":
-                ch, bt = divmod(a, NBT)
                 o = opool.tile([P, 256, 2], F32, name="o", tag="o")
-                leave("F%d" % a, o[:], live[("f", a)][:].rearrange("p e j -> p j e"))
+                if n_exit % 2 == 0:
+                    nc.scalar.copy(out=o[:], in_=f[:].rearrange("p e j -> p j e"))
+                else:
+                    nc.vector.tensor_copy(out=o[:], in_=f[:].rearrange("p e j -> p j e"))
+                n_exit += 1
                 nc.sync.dma_start(
-                    out=out[bt * P : (bt + 1) * P, ch * 512 : (ch + 1) * 512], in_=o[:].rearrange("p j e -> p (j e)")
+                    out=out[bt * P : (bt + 1) * P, ch * 512 : (ch + 1) * 512],
+                    in_=o[:].rearrange("p j e -> p (j e)"),
                 )
-            else:
-                assert False, kind
-
-        for op in ORDER:
-            run(op)

@@ -22,7 +22,7 @@ NBT = B // P
 FLOPS = 2 * B * MID * MID + 2 * B * MID * HALF
 
 LOOKAHEAD = 12
-NV_W = 264
+NV_W = 200
 
 
 def regroup(nc, dst, src, width, nv):
@@ -70,10 +70,12 @@ def tile_additivecoupling_pa_kernel(tc, x, h3, W4, b4, W5, b5, out):
         def load_w4(i):
             c2, g = divmod(i, NG)
             r = raw4.tile([P, 4, KP], BF16, name="w4r", tag="w4r")
-            nc.sync.dma_start(
-                out=r[:],
-                in_=W4[g * KP : (g + 1) * KP, c2 * KP : (c2 + 1) * KP].rearrange("(p j) c -> p j c", j=4),
-            )
+            for u in range(2):
+                k0 = g * KP + u * 256
+                nc.sync.dma_start(
+                    out=r[:, 2 * u : 2 * u + 2, :],
+                    in_=W4[k0 : k0 + 256, c2 * KP : (c2 + 1) * KP].rearrange("(q e) c -> q e c", e=2),
+                )
             w4r[i] = r
 
         for i in range(LOOKAHEAD):
@@ -89,22 +91,23 @@ def tile_additivecoupling_pa_kernel(tc, x, h3, W4, b4, W5, b5, out):
                     out=t_[:], in_=W5[c * KP : (c + 1) * KP, :].rearrange("(t p) j -> p t j", p=P)
                 )
                 w5r.append(t_)
-            xall = keep.tile([P, NBT, 2 * HALF], BF16, name="xall")
-            nc.sync.dma_start(out=xall[:], in_=x.rearrange("(bt p) c -> p bt c", p=P))
             for bt in range(NBT):
-                xr.append(xall[:, bt, :])
+                t_ = keep.tile([P, 2 * HALF], BF16, name="xr%d" % bt)
+                nc.sync.dma_start(out=t_[:], in_=x[bt * P : (bt + 1) * P, :])
+                xr.append(t_)
 
         h3g = keep.tile([P, NG, B, 2], F32, name="h3g", align_bytes=64)
         h3c = keep.tile([P, NG, B], U32, name="h3c", align_bytes=64)
         h3s = keep.tile([P, NG, B], U8, name="h3s", align_bytes=64)
         n_exit = 0
         for bt in range(NBT):
-            words = h3r[bt][:].bitcast(F32).rearrange("p (g q u) -> p g u q", g=NG, u=2)
+            words = h3r[bt][:].bitcast(F32)
             for gp in range(2):
                 pt = psa.tile([P, 2, 2, P], F32, name="pt", tag="a")
                 for gg in range(2):
                     for u in range(2):
-                        nc.tensor.transpose(pt[:, gg, u, :], words[:, 2 * gp + gg, u, :], ident[:])
+                        w0 = (2 * gp + gg) * 256 + u * P
+                        nc.tensor.transpose(pt[:, gg, u, :], words[:, w0 : w0 + P], ident[:])
                 dst = h3g[:, 2 * gp : 2 * gp + 2, bt * P : (bt + 1) * P, :]
                 src = pt[:].rearrange("p g u b -> p g b u")
                 if n_exit % 2 == 0:

@@ -22,7 +22,7 @@ NBT = B // P
 FLOPS = 2 * B * MID * MID + 2 * B * MID * HALF
 
 LOOKAHEAD = 12
-NV_W = 200
+NV_W = 312
 
 
 def regroup(nc, dst, src, width, nv):

from contextlib import ExitStack

import concourse.mybir as mybir
from concourse.masks import make_identity

F32 = mybir.dt.float32
BF16 = mybir.dt.bfloat16
U32 = mybir.dt.uint32
U8 = mybir.dt.uint8
FP8X4 = mybir.dt.float8_e4m3fn_x4
ACT = mybir.ActivationFunctionType
ALU = mybir.AluOpType

P = 128
B = 512
MID = 2048
HALF = 512
KP = 512
NG = MID // KP
NBT = B // P

FLOPS = 2 * B * MID * MID + 2 * B * MID * HALF

LOOKAHEAD = 12
NV_W = 312


def regroup(nc, dst, src, width, nv):
    nc.vector.tensor_copy(
        out=dst[:, 0:nv, :].rearrange("p (c i) t -> p c t i", i=4),
        in_=src[:, :, 0:nv].rearrange("p t (c i) -> p c t i", i=4),
    )
    if nv < width:
        nc.scalar.copy(
            out=dst[:, nv:width, :].rearrange("p (c i) t -> p c t i", i=4),
            in_=src[:, :, nv:width].rearrange("p t (c i) -> p c t i", i=4),
        )


def tile_additivecoupling_pa_kernel(tc, x, h3, W4, b4, W5, b5, out):
    nc = tc.nc
    with ExitStack() as ctx:
        const = ctx.enter_context(tc.tile_pool(name="const", bufs=1))
        keep = ctx.enter_context(tc.tile_pool(name="keep", bufs=1))
        raw4 = ctx.enter_context(tc.tile_pool(name="raw4", bufs=LOOKAHEAD))
        grp = ctx.enter_context(tc.tile_pool(name="grp", bufs=4))
        cod4 = ctx.enter_context(tc.tile_pool(name="cod4", bufs=6))
        h4pool = ctx.enter_context(tc.tile_pool(name="h4pool", bufs=2))
        opool = ctx.enter_context(tc.tile_pool(name="opool", bufs=8))
        psa = ctx.enter_context(tc.psum_pool(name="psa", bufs=8))

        ident = const.tile([P, P], F32, name="ident")
        make_identity(nc, ident[:])
        identb = const.tile([P, P], BF16, name="identb")
        nc.vector.tensor_copy(out=identb[:], in_=ident[:])

        brow = const.tile([P, P], BF16, name="brow")
        nc.vector.memset(brow[:], 0.0)
        nc.sync.dma_start(out=brow[0:16, :], in_=b4.rearrange("(r c) -> r c", c=P))
        nc.sync.dma_start(out=brow[16:20, :], in_=b5.rearrange("(r c) -> r c", c=P))

        h3r = []
        for bt in range(NBT):
            t_ = keep.tile([P, MID], BF16, name="h3r%d" % bt)
            nc.sync.dma_start(out=t_[:], in_=h3[bt * P : (bt + 1) * P, :])
            h3r.append(t_)

        w4r = {}

        def load_w4(i):
            c2, g = divmod(i, NG)
            r = raw4.tile([P, 4, KP], BF16, name="w4r", tag="w4r")
            for u in range(2):
                k0 = g * KP + u * 256
                nc.sync.dma_start(
                    out=r[:, 2 * u : 2 * u + 2, :],
                    in_=W4[k0 : k0 + 256, c2 * KP : (c2 + 1) * KP].rearrange("(q e) c -> q e c", e=2),
                )
            w4r[i] = r

        for i in range(LOOKAHEAD):
            load_w4(i)

        w5r = []
        xr = []

        def load_tail():
            for c in range(NG):
                t_ = keep.tile([P, 4, HALF], BF16, name="w5r%d" % c)
                nc.sync.dma_start(
                    out=t_[:], in_=W5[c * KP : (c + 1) * KP, :].rearrange("(t p) j -> p t j", p=P)
                )
                w5r.append(t_)
            for bt in range(NBT):
                t_ = keep.tile([P, 2 * HALF], BF16, name="xr%d" % bt)
                nc.sync.dma_start(out=t_[:], in_=x[bt * P : (bt + 1) * P, :])
                xr.append(t_)

        h3g = keep.tile([P, NG, B, 2], F32, name="h3g", align_bytes=64)
        h3c = keep.tile([P, NG, B], U32, name="h3c", align_bytes=64)
        h3s = keep.tile([P, NG, B], U8, name="h3s", align_bytes=64)
        n_exit = 0
        for bt in range(NBT):
            words = h3r[bt][:].bitcast(F32)
            for gp in range(2):
                pt = psa.tile([P, 2, 2, P], F32, name="pt", tag="a")
                for gg in range(2):
                    for u in range(2):
                        w0 = (2 * gp + gg) * 256 + u * P
                        nc.tensor.transpose(pt[:, gg, u, :], words[:, w0 : w0 + P], ident[:])
                dst = h3g[:, 2 * gp : 2 * gp + 2, bt * P : (bt + 1) * P, :]
                src = pt[:].rearrange("p g u b -> p g b u")
                if n_exit % 2 == 0:
                    nc.scalar.copy(out=dst, in_=src)
                else:
                    nc.vector.tensor_copy(out=dst, in_=src)
                n_exit += 1
        for g in range(NG):
            nc.vector.quantize_mx(
                out=h3c[:, g, :].bitcast(FP8X4),
                scales=h3s[:, g, :],
                in_=h3g[:, g, :, :].rearrange("p b u -> p (b u)").bitcast(BF16),
            )

        browf = const.tile([P, P], F32, name="browf")
        nc.vector.tensor_copy(out=browf[:], in_=brow[:])
        pb = psa.tile([P, 512], F32, name="pb", tag="a")
        nc.tensor.transpose(pb[:, 0:P], browf[:], ident[:])
        bias = const.tile([P, 32], F32, name="bias")
        nc.vector.tensor_copy(out=bias[:, 0:20], in_=pb[:, 0:20])

        w4g = {}
        ps1 = {}
        h4p = {}
        h4g = {}
        h4c = [keep.tile([P, B], U32, name="h4c%d" % c, align_bytes=64) for c in range(NG)]
        h4s = [keep.tile([P, B], U8, name="h4s%d" % c, align_bytes=64) for c in range(NG)]

        def stage_a(i):
            g_ = grp.tile([P, KP, 4], BF16, name="wg", tag="g", align_bytes=64)
            regroup(nc, g_, w4r[i], KP, NV_W)
            w4g[i] = g_

        def stage_b(i):
            c2, g = divmod(i, NG)
            codes = cod4.tile([P, KP], U32, name="w4c", tag="w4c", align_bytes=64)
            scales = cod4.tile([P, KP], U8, name="w4s", tag="w4s", align_bytes=64)
            nc.vector.quantize_mx(
                out=codes[:].bitcast(FP8X4),
                scales=scales[:],
                in_=w4g[i][:].rearrange("p c t -> p (c t)"),
            )
            for t in range(4):
                if g == 0:
                    ps1[t] = psa.tile([P, B], F32, name="ps1", tag="a")
                nc.tensor.matmul_mx(
                    out=ps1[t][:],
                    lhsT=codes[:, t * P : (t + 1) * P].bitcast(FP8X4),
                    lhsT_scale=scales[:, t * P : (t + 1) * P],
                    rhs=h3c[:, g, :].bitcast(FP8X4),
                    rhs_scale=h3s[:, g, :],
                    start=(g == 0),
                    stop=(g == NG - 1),
                )

        def stage_c(c2, on_vector):
            hp = h4pool.tile([P, 4, B], BF16, name="h4p", tag="h4p")
            for t in range(4):
                col = bias[:, 4 * c2 + t : 4 * c2 + t + 1]
                if t in on_vector:
                    nc.vector.tensor_scalar(
                        out=hp[:, t, :], in0=ps1[t][:], scalar1=col, scalar2=0.0, op0=ALU.add, op1=ALU.max
                    )
                else:
                    nc.scalar.activation(out=hp[:, t, :], in_=ps1[t][:], func=ACT.Relu, bias=col, scale=1.0)
            h4p[c2] = hp

        def stage_d(c2, nv):
            hg = h4pool.tile([P, B, 4], BF16, name="h4g", tag="h4g", align_bytes=64)
            regroup(nc, hg, h4p[c2], B, nv)
            h4g[c2] = hg

        def stage_e(c2):
            nc.vector.quantize_mx(
                out=h4c[c2][:].bitcast(FP8X4),
                scales=h4s[c2][:],
                in_=h4g[c2][:].rearrange("p b t -> p (b t)"),
            )

        for i in range(4 * NG + 1):
            if i < 4 * NG:
                stage_a(i)
                if i + LOOKAHEAD < 4 * NG:
                    load_w4(i + LOOKAHEAD)
                if i + LOOKAHEAD == 4 * NG - 1:
                    load_tail()
            if i >= 6 and i % 4 == 2:
                stage_d(i // 4 - 1, B)
            if i >= 1:
                stage_b(i - 1)
                if (i - 1) % 4 == 3:
                    last = i == 4 * NG
                    stage_c((i - 1) // 4, (1, 3) if last else ())
            if i >= 7 and i % 4 == 3:
                stage_e(i // 4 - 1)

        w5c = keep.tile([P, NG, HALF], U32, name="w5c", align_bytes=64)
        w5s = keep.tile([P, NG, HALF], U8, name="w5s", align_bytes=64)
        w5g = {}

        def stage_a5(c):
            g_ = grp.tile([P, HALF, 4], BF16, name="wg5", tag="g", align_bytes=64)
            regroup(nc, g_, w5r[c], HALF, NV_W)
            w5g[c] = g_

        def stage_q5(c):
            nc.vector.quantize_mx(
                out=w5c[:, c, :].bitcast(FP8X4),
                scales=w5s[:, c, :],
                in_=w5g[c][:].rearrange("p c t -> p (c t)"),
            )

        stage_a5(0)
        stage_a5(1)
        stage_d(3, 320)
        stage_q5(0)
        stage_a5(2)
        stage_e(3)
        stage_q5(1)
        stage_a5(3)
        stage_q5(2)
        stage_q5(3)

        acc = [psa.tile([P, B], F32, name="acc%d" % jt, tag="a") for jt in range(4)]
        for c in range(NG):
            for jt in range(4):
                nc.tensor.matmul_mx(
                    out=acc[jt][:],
                    lhsT=w5c[:, c, jt * P : (jt + 1) * P].bitcast(FP8X4),
                    lhsT_scale=w5s[:, c, jt * P : (jt + 1) * P],
                    rhs=h4c[c][:].bitcast(FP8X4),
                    rhs_scale=h4s[c][:],
                    start=(c == 0),
                    stop=(c == NG - 1),
                )

        zt = []
        for jt in range(4):
            z = keep.tile([P, B], F32, name="zt%d" % jt)
            col = bias[:, 16 + jt : 17 + jt]
            if jt % 2 == 0:
                nc.scalar.activation(out=z[:], in_=acc[jt][:], func=ACT.Identity, bias=col, scale=1.0)
            else:
                nc.vector.tensor_scalar(out=z[:], in0=acc[jt][:], scalar1=col, scalar2=None, op0=ALU.add)
            zt.append(z)
        n_exit = 0
        for ch in range(2):
            for bt in range(NBT):
                f = psa.tile([P, 2, 256], F32, name="f", tag="a")
                nc.tensor.matmul(
                    out=f[:],
                    lhsT=identb[:],
                    rhs=xr[bt][:, ch * 512 : (ch + 1) * 512].rearrange("p (j e) -> p e j", e=2),
                    start=True,
                    stop=False,
                )
                for r in range(2):
                    nc.tensor.matmul(
                        out=f[:, 0, r * P : (r + 1) * P],
                        lhsT=zt[2 * ch + r][:, bt * P : (bt + 1) * P],
                        rhs=ident[:],
                        is_transpose=True,
                        start=False,
                        stop=(r == 1),
                    )
                o = opool.tile([P, 256, 2], F32, name="o", tag="o")
                if n_exit % 2 == 0:
                    nc.scalar.copy(out=o[:], in_=f[:].rearrange("p e j -> p j e"))
                else:
                    nc.vector.tensor_copy(out=o[:], in_=f[:].rearrange("p e j -> p j e"))
                n_exit += 1
                nc.sync.dma_start(
                    out=out[bt * P : (bt + 1) * P, ch * 512 : (ch + 1) * 512],
                    in_=o[:].rearrange("p j e -> p (j e)"),
                )
